import numpy as np
import ml_dtypes


def mxq(x, axis, fmt="e4m3"):
    dtype, down = {"e4m3": (ml_dtypes.float8_e4m3fn, 7), "e5m2": (ml_dtypes.float8_e5m2, 14)}[fmt]
    v = np.moveaxis(np.asarray(x, np.float32).astype(ml_dtypes.bfloat16).astype(np.float64), axis, -1)
    blocks = v.reshape(v.shape[:-1] + (-1, 32))
    amax = np.abs(blocks).max(-1, keepdims=True)
    byte = np.maximum(np.where(amax > 0, np.frexp(amax)[1] - 1 + 127, 0) - down, 1)
    scale = np.exp2(byte - 127.0)
    codes = (blocks / scale).astype(np.float32).astype(dtype).astype(np.float64)
    return np.moveaxis((codes * scale).reshape(v.shape), -1, axis)


WIDE = False


def mx_kscale(k):
    if not WIDE:
        return np.ones(k)
    levels = np.array([10, -10, 5, -5, 0])
    if k % 512:
        return np.exp2(np.random.permutation(np.resize(levels, k // 32))).repeat(32)
    a = np.empty((k // 512, 16))
    for p in range(k // 512):
        a[p, :8] = np.random.permutation(np.resize(levels, 8))
        for g in range(8):
            far = levels[np.abs(levels - a[p, g]) >= 10]
            a[p, g + 8] = far[np.random.randint(len(far))]
    return np.exp2(a.ravel()).repeat(32)


BF16 = ml_dtypes.bfloat16


def bf(x):
    return np.asarray(x, np.float32).astype(BF16)


def f64(x):
    return np.asarray(x).astype(np.float64)


B, N, SIZE, CH = 4096, 16, 512, 256


def sigmoid(v):
    return 1.0 / (1.0 + np.exp(-v))


def setup_inputs():
    s = mx_kscale(SIZE)
    d = {"z0": bf(np.random.standard_normal((B, SIZE)) * s),
         "h_tilde": bf(np.random.standard_normal((B, CH)) * np.sqrt(N)),
         "fc_sum": bf(np.random.standard_normal((B, CH)) * 1.2)}
    for g in ("i", "o", "u"):
        d["W_" + g] = bf(np.random.standard_normal((CH, SIZE)) / np.sqrt(SIZE) / s)
        d["U_" + g] = bf(np.random.standard_normal((CH, CH)) / np.sqrt(CH * N))
        d["b_" + g] = bf(np.random.standard_normal(CH) * 0.5)
    return d


def reference(z0, h_tilde, fc_sum, W_i, U_i, b_i, W_o, U_o, b_o, W_u, U_u, b_u):
    zq = mxq(f64(z0), 1, "e4m3")
    ht = f64(h_tilde)
    i_j = sigmoid((zq @ mxq(f64(W_i), 1, "e4m3").T) + ht @ f64(U_i).T + f64(b_i))
    o_j = sigmoid((zq @ mxq(f64(W_o), 1, "e4m3").T) + ht @ f64(U_o).T + f64(b_o))
    u_j = np.tanh((zq @ mxq(f64(W_u), 1, "e4m3").T) + ht @ f64(U_u).T + f64(b_u))
    c_j = i_j * u_j + f64(fc_sum)
    h_j = o_j * np.tanh(c_j)
    return np.concatenate([h_j, c_j], axis=-1)

@@ -1,0 +1,391 @@
+from contextlib import ExitStack
+
+import concourse.mybir as mybir
+from concourse.masks import make_identity
+
+F32 = mybir.dt.float32
+BF16 = mybir.dt.bfloat16
+U32 = mybir.dt.uint32
+U8 = mybir.dt.uint8
+I32 = mybir.dt.int32
+FP8X4 = mybir.dt.float8_e4m3fn_x4
+ACT = mybir.ActivationFunctionType
+ALU = mybir.AluOpType
+
+P = 128
+NODES, SIZE, CH = 4096, 512, 256
+TILES = NODES // P
+GROUP = 4
+GROUPS = TILES // GROUP
+PAIRS = TILES // 2
+BANK = 512
+FILLS = 6 * PAIRS
+RING = 5
+LEAD = RING - 1
+HEAD_GROUPS = 3
+HEAD_FILLS = 9
+FIRST_TENSOR_BIAS = 2
+GPSIMD_H = 2
+FLOPS = 2 * NODES * (SIZE + CH) * 3 * CH
+
+
+def tile_treelstm_pb_t_kernel(
+    tc, z0, h_tilde, fc_sum, W_i, U_i, b_i, W_o, U_o, b_o, W_u, U_u, b_u, out
+):
+    nc = tc.nc
+    with ExitStack() as ctx:
+        ctx.enter_context(tc.manual_schedule())
+        keep = ctx.enter_context(tc.tile_pool(name="keep", bufs=1))
+        front = ctx.enter_context(tc.tile_pool(name="front", bufs=3))
+        io_pool = ctx.enter_context(tc.tile_pool(name="io", bufs=4))
+        u_pool = ctx.enter_context(tc.tile_pool(name="u", bufs=3))
+        res_pool = ctx.enter_context(tc.tile_pool(name="res", bufs=4))
+        tanh_pool = ctx.enter_context(tc.tile_pool(name="tanh", bufs=3))
+        turn_psum = ctx.enter_context(tc.psum_pool(name="turn", bufs=8 - RING))
+        sum_psum = ctx.enter_context(tc.psum_pool(name="sums", bufs=RING))
+
+        z_dram = z0.rearrange("(p t) k -> p t k", t=TILES)
+        h_dram = h_tilde.rearrange("(p t) k -> p t k", t=TILES)
+        fc_dram = fc_sum.rearrange("(p t) k -> p t k", t=TILES)
+        out_dram = out.rearrange("(p t) c -> p t c", t=TILES)
+
+        bias_rows = keep.tile([P, 3 * CH], BF16, name="bias_rows")
+        nc.vector.memset(bias_rows[:].bitcast(I32), 0)
+        for j, b in enumerate((b_i, b_o, b_u)):
+            nc.scalar.dma_start(
+                out=bias_rows[0:1, CH * j : CH * (j + 1)], in_=b.rearrange("(o n) -> o n", o=1)
+            )
+        identity = keep.tile([P, P], F32, name="identity")
+        make_identity(nc, identity[:])
+        ones = keep.tile([P, P], BF16, name="ones")
+        nc.vector.memset(ones[:], 1.0)
+        warm = keep.tile([P, 8], F32, name="warm")
+        nc.vector.memset(warm[:], 0.0)
+        nc.scalar.activation(out=warm[:], in_=warm[:], func=ACT.Sigmoid)
+
+        z_in = [keep.tile([P, GROUP, SIZE], BF16, name="z_in%d" % g) for g in range(GROUPS)]
+        h_in = [keep.tile([P, GROUP, CH], BF16, name="h_in%d" % g) for g in range(GROUPS)]
+        fc_in = [keep.tile([P, GROUP, CH], BF16, name="fc_in%d" % g) for g in range(GROUPS)]
+        w_in = [keep.tile([P, 2, SIZE], BF16, name="w_in%d" % j) for j in range(3)]
+        u_in = [keep.tile([P, 2, CH], BF16, name="u_in%d" % j) for j in range(3)]
+
+        def load(dst, src, g, t0=0, t1=GROUP):
+            nc.sync.dma_start(out=dst[g][:, t0:t1, :], in_=src[:, GROUP * g + t0 : GROUP * g + t1, :])
+
+        def load_weight(dst, src):
+            nc.sync.dma_start(out=dst[:], in_=src.rearrange("(b p) k -> p b k", p=P))
+
+        load_weight(u_in[0], U_i)
+        load_weight(u_in[1], U_o)
+        load(h_in, h_dram, 0)
+        load_weight(u_in[2], U_u)
+        load_weight(w_in[0], W_i)
+        load_weight(w_in[1], W_o)
+        load(z_in, z_dram, 0, 0, 2)
+        load_weight(w_in[2], W_u)
+        load(z_in, z_dram, 0, 2, 4)
+        for g in range(1, GROUPS):
+            load(z_in, z_dram, g)
+            load(h_in, h_dram, g)
+            if g >= 2:
+                load(fc_in, fc_dram, g - 2)
+        load(fc_in, fc_dram, GROUPS - 2)
+        load(fc_in, fc_dram, GROUPS - 1)
+
+        def words(tile_ap):
+            return tile_ap[:].rearrange("p a k -> p (a k)").bitcast(F32)
+
+        def turn(bank, at, src_words, square):
+            nc.tensor.transpose(
+                bank[:, P * at : P * (at + 1)], src_words[:, P * square : P * (square + 1)], identity[:]
+            )
+
+        def turn_mx(bank, at, src_words):
+            w0 = 2 * P * (at // 2) + at % 2
+            nc.tensor.transpose(
+                bank[:, P * (at % 4) : P * (at % 4 + 1)], src_words[:, w0 : w0 + 2 * P - 1 : 2], identity[:]
+            )
+
+        h_bank, z_bank = {}, {}
+
+        def turn_h(g, j):
+            if j == 0:
+                h_bank[g] = turn_psum.tile([P, BANK], F32, name="h_bank%d" % g, tag="turn")
+            turn(h_bank[g], j, words(h_in[g]), j)
+
+        def turn_z(g, half, j):
+            if j == 0:
+                z_bank[g, half] = turn_psum.tile([P, BANK], F32, name="z_bank%d_%d" % (g, half), tag="turn")
+            turn_mx(z_bank[g, half], 4 * half + j, words(z_in[g]))
+
+        def regroup(dst_words, bank):
+            nc.scalar.copy(
+                out=dst_words.rearrange("p (s m v) -> p s m v", s=2, m=P, v=2),
+                in_=bank[:].rearrange("p (s v m) -> p s m v", s=2, v=2, m=P),
+            )
+
+        hT, z_grouped, z_codes, z_scales = {}, {}, {}, {}
+
+        def copy_h(g):
+            hT[g] = front.tile([P, BANK], F32, name="hT%d" % g, tag="hT")
+            nc.scalar.copy(out=hT[g][:], in_=h_bank[g][:])
+
+        def regroup_z(g, half):
+            if half == 0:
+                z_grouped[g] = front.tile(
+                    [P, 4 * BANK], BF16, name="z_grouped%d" % g, tag="zg", align_bytes=64
+                )
+            regroup(z_grouped[g][:].bitcast(F32)[:, BANK * half : BANK * (half + 1)], z_bank[g, half])
+
+        def quantise_z(g, half0=0, half1=2):
+            if half0 == 0:
+                z_codes[g] = front.tile([P, BANK], U32, name="z_codes%d" % g, tag="zc", align_bytes=64)
+                z_scales[g] = front.tile([P, BANK], U8, name="z_scales%d" % g, tag="zs", align_bytes=64)
+            nc.vector.quantize_mx(
+                out=z_codes[g][:, 2 * P * half0 : 2 * P * half1].bitcast(FP8X4),
+                scales=z_scales[g][:, 2 * P * half0 : 2 * P * half1],
+                in_=z_grouped[g][:, 8 * P * half0 : 8 * P * half1],
+            )
+
+        def front_h(g):
+            for j in range(GROUP):
+                turn_h(g, j)
+            copy_h(g)
+
+        def front_z(g, half):
+            for j in range(4):
+                turn_z(g, half, j)
+            regroup_z(g, half)
+
+        def ride(pair, j):
+            g = pair // 2 + 2
+            if HEAD_GROUPS <= g < GROUPS:
+                turn_z(g, pair % 2, j)
+                if pair % 2 == 1:
+                    turn_h(g, j)
+
+        uT_words = keep.tile([P, 3 * CH], F32, name="uT_words")
+        uT = uT_words[:].bitcast(BF16).rearrange("p (n e) -> p n e", e=2)
+        bias_all = keep.tile([P, 2 * BANK], F32, name="bias_all")
+        w_grouped = keep.tile([P, 12 * CH], BF16, name="w_grouped", align_bytes=64)
+        w_codes = keep.tile([P, 3 * CH], U32, name="w_codes", align_bytes=64)
+        w_scales = keep.tile([P, 3 * CH], U8, name="w_scales", align_bytes=64)
+
+        def front_w(j):
+            bank = sum_psum.tile([P, BANK], F32, name="w_bank%d" % j, tag="sum")
+            for square in range(4):
+                turn_mx(bank, square, words(w_in[j]))
+            regroup(w_grouped[:].bitcast(F32)[:, BANK * j : BANK * (j + 1)], bank)
+
+        def quantise_w(c0, c1):
+            nc.vector.quantize_mx(
+                out=w_codes[:, c0:c1].bitcast(FP8X4), scales=w_scales[:, c0:c1], in_=w_grouped[:, 4 * c0 : 4 * c1]
+            )
+
+        sums, gates_io, gates_u = {}, {}, {}
+
+        def tensor_bias(pair):
+            return pair >= FIRST_TENSOR_BIAS
+
+        def tensor_fill(n):
+            pair, k = divmod(n, 6)
+            g, second = divmod(pair, 2)
+            sums[n] = sum_psum.tile([P, BANK], F32, name="sums%d" % n, tag="sum")
+            if k % 3 < 2:
+                parts = [(2 * second + k % 3, 0, BANK, 0)]
+            else:
+                parts = [(2 * second, BANK, 3 * CH, 0), (2 * second + 1, BANK, 3 * CH, CH)]
+            for t, c0, c1, at in parts:
+                dst = sums[n][:, at : at + c1 - c0]
+                if k >= 3:
+                    nc.tensor.matmul_mx(
+                        out=dst,
+                        lhsT=z_codes[g][:, P * t : P * (t + 1)].bitcast(FP8X4),
+                        lhsT_scale=z_scales[g][:, P * t : P * (t + 1)],
+                        rhs=w_codes[:, c0:c1].bitcast(FP8X4),
+                        rhs_scale=w_scales[:, c0:c1],
+                        start=True,
+                        stop=True,
+                    )
+                    continue
+                h_tile = hT[g][:].bitcast(BF16).rearrange("p (t m e) -> p t m e", t=GROUP, m=P, e=2)
+                with_bias = k == 2 and tensor_bias(pair)
+                for e in range(2):
+                    nc.tensor.matmul(
+                        out=dst,
+                        lhsT=h_tile[:, t, :, e],
+                        rhs=uT[:, c0:c1, e],
+                        start=(e == 0),
+                        stop=(e == 1 and not with_bias),
+                    )
+                    if k < 2:
+                        ride(pair, 2 * k + e)
+                if with_bias:
+                    nc.tensor.matmul(out=dst, lhsT=ones[:], rhs=bias_rows[:, c0:c1], start=False, stop=True)
+
+        def gate_slice(pair, k):
+            g, second = divmod(pair, 2)
+            if g not in gates_io:
+                gates_io[g] = io_pool.tile([P, GROUP * BANK], F32, name="gates_io%d" % g, tag="io")
+                gates_u[g] = u_pool.tile([P, GROUP * CH], F32, name="gates_u%d" % g, tag="u")
+            if k % 3 < 2:
+                t = 2 * second + k % 3
+                return gates_io[g][:, BANK * t : BANK * (t + 1)]
+            return gates_u[g][:, BANK * second : BANK * (second + 1)]
+
+        def vector_empty(n):
+            pair, k = divmod(n, 6)
+            if k == 2 and tensor_bias(pair):
+                return
+            dst = gate_slice(pair, k)
+            if k >= 3:
+                other = dst
+            else:
+                other = bias_all[:, 0:BANK] if k < 2 else bias_all[:, BANK : 2 * BANK]
+            nc.vector.tensor_tensor(out=dst, in0=sums[n][:], in1=other, op=ALU.add)
+
+        def scalar_empty(pair):
+            nc.scalar.copy(out=gate_slice(pair, 2), in_=sums[6 * pair + 2][:])
+
+        def sigmoid_io(pair):
+            g, second = divmod(pair, 2)
+            v = gates_io[g][:, 2 * BANK * second : 2 * BANK * (second + 1)]
+            nc.scalar.activation(out=v, in_=v, func=ACT.Sigmoid)
+
+        def tanh_u(pair):
+            v = gate_slice(pair, 2)
+            nc.scalar.activation(out=v, in_=v, func=ACT.Tanh)
+
+        res, tanh_c_sb = {}, {}
+
+        def cell(engine, g, t0, t1):
+            if g not in res:
+                res[g] = res_pool.tile([P, GROUP, 2 * CH], F32, name="res%d" % g, tag="res")
+                tanh_c_sb[g] = tanh_pool.tile([P, GROUP, CH], F32, name="tanh_c%d" % g, tag="tanh")
+            io = gates_io[g][:].rearrange("p (t c) -> p t c", c=BANK)
+            uu = gates_u[g][:].rearrange("p (t c) -> p t c", c=CH)
+            c = res[g][:, t0:t1, CH : 2 * CH]
+            engine.tensor_tensor(out=c, in0=io[:, t0:t1, 0:CH], in1=uu[:, t0:t1, :], op=ALU.mult)
+            engine.tensor_tensor(out=c, in0=c, in1=fc_in[g][:, t0:t1, :], op=ALU.add)
+            store(g, t0, t1, CH, 2 * CH)
+
+        def tanh_c(g, t0, t1):
+            nc.scalar.activation(
+                out=tanh_c_sb[g][:, t0:t1, :], in_=res[g][:, t0:t1, CH : 2 * CH], func=ACT.Tanh
+            )
+
+        def hidden(engine, g, t0, t1):
+            io = gates_io[g][:].rearrange("p (t c) -> p t c", c=BANK)
+            engine.tensor_tensor(
+                out=res[g][:, t0:t1, 0:CH], in0=io[:, t0:t1, CH:BANK], in1=tanh_c_sb[g][:, t0:t1, :], op=ALU.mult
+            )
+
+        def store(g, t0, t1, c0, c1):
+            nc.sync.dma_start(
+                out=out_dram[:, GROUP * g + t0 : GROUP * g + t1, c0:c1], in_=res[g][:, t0:t1, c0:c1]
+            )
+
+        def after_pair(pair):
+            g, second = divmod(pair, 2)
+            if pair + 1 < PAIRS and tensor_bias(pair + 1):
+                scalar_empty(pair + 1)
+            ahead = g + 2
+            if not second:
+                if HEAD_GROUPS <= ahead < GROUPS:
+                    regroup_z(ahead, 1)
+                return
+            if HEAD_GROUPS <= ahead < GROUPS:
+                copy_h(ahead)
+            if HEAD_GROUPS <= ahead + 1 < GROUPS:
+                regroup_z(ahead + 1, 0)
+            if g < GROUPS - 1:
+                cell(nc.gpsimd, g, 0, GROUP)
+            if g >= 1:
+                tanh_c(g - 1, 0, GROUP)
+                if g < GROUPS - 1:
+                    hidden(nc.gpsimd, g - 1, 0, GPSIMD_H)
+            if ahead < GROUPS:
+                quantise_z(ahead)
+            if g >= 2:
+                hidden(nc.vector, g - 2, GPSIMD_H, GROUP)
+                store(g - 2, 0, GROUP, 0, CH)
+
+        u_bank = [sum_psum.tile([P, BANK], F32, name="u_bank%d" % j, tag="sum") for j in range(2)]
+        for j in range(2):
+            for b in range(2):
+                turn(u_bank[0], 2 * j + b, words(u_in[j]), b)
+        nc.vector.tensor_copy(out=uT_words[:, 0:BANK], in_=u_bank[0][:])
+        front_h(0)
+        for b in range(2):
+            turn(u_bank[1], b, words(u_in[2]), b)
+        nc.vector.tensor_copy(out=uT_words[:, BANK : 3 * CH], in_=u_bank[1][:, 0:CH])
+        bias_io = sum_psum.tile([P, BANK], F32, name="bias_io", tag="sum")
+        nc.tensor.matmul(out=bias_io[:], lhsT=ones[:], rhs=bias_rows[:, 0:BANK], start=True, stop=True)
+        bias_uu = sum_psum.tile([P, BANK], F32, name="bias_uu", tag="sum")
+        for j in range(2):
+            nc.tensor.matmul(
+                out=bias_uu[:, CH * j : CH * (j + 1)],
+                lhsT=ones[:],
+                rhs=bias_rows[:, BANK : 3 * CH],
+                start=True,
+                stop=True,
+            )
+        nc.scalar.copy(out=bias_all[:, 0:BANK], in_=bias_io[:])
+        nc.vector.tensor_copy(out=bias_all[:, BANK : 2 * BANK], in_=bias_uu[:])
+
+        def plain_fill(n):
+            tensor_fill(n)
+            vector_empty(n)
+
+        plain_fill(0)
+        front_w(0)
+        plain_fill(1)
+        front_w(1)
+        front_z(0, 0)
+        plain_fill(2)
+        quantise_w(0, BANK)
+        front_w(2)
+        quantise_z(0, 0, 1)
+        plain_fill(6)
+        quantise_w(BANK, 3 * CH)
+        front_z(0, 1)
+        plain_fill(7)
+        quantise_z(0, 1, 2)
+        plain_fill(8)
+        front_h(1)
+        front_z(1, 0)
+        front_z(1, 1)
+        for n in (3, 4, 5):
+            tensor_fill(n)
+        for n in (3, 4, 5):
+            vector_empty(n)
+        quantise_z(1)
+        front_z(2, 0)
+        front_z(2, 1)
+        front_h(2)
+        sigmoid_io(0)
+        tanh_u(0)
+        after_pair(0)
+
+        for n in range(HEAD_FILLS, FILLS + LEAD):
+            if n < FILLS:
+                tensor_fill(n)
+            if n - LEAD < HEAD_FILLS:
+                continue
+            pair, k = divmod(n - LEAD, 6)
+            vector_empty(n - LEAD)
+            if k == 4:
+                sigmoid_io(pair)
+            if k == 5:
+                tanh_u(pair)
+                after_pair(pair)
+
+        last = GROUPS - 1
+        for t0 in (0, 2):
+            cell(nc.vector, last, t0, t0 + 2)
+            tanh_c(last, t0, t0 + 2)
+        hidden(nc.vector, last - 1, 0, GROUP)
+        store(last - 1, 0, GROUP, 0, CH)
+        for t0 in (0, 2):
+            hidden(nc.vector, last, t0, t0 + 2)
+            store(last, t0, t0 + 2, 0, CH)

@@ -19,12 +19,10 @@ GROUP = 4
 GROUPS = TILES // GROUP
 PAIRS = TILES // 2
 BANK = 512
-FILLS = 6 * PAIRS
+U_BLOCKS = CH // P
 RING = 5
 LEAD = RING - 1
 HEAD_GROUPS = 3
-HEAD_FILLS = 9
-FIRST_TENSOR_BIAS = 2
 GPSIMD_H = 2
 FLOPS = 2 * NODES * (SIZE + CH) * 3 * CH
 
@@ -39,6 +37,7 @@ def tile_treelstm_pb_t_kernel(
         front = ctx.enter_context(tc.tile_pool(name="front", bufs=3))
         io_pool = ctx.enter_context(tc.tile_pool(name="io", bufs=4))
         u_pool = ctx.enter_context(tc.tile_pool(name="u", bufs=3))
+        u_mx_pool = ctx.enter_context(tc.tile_pool(name="u_mx", bufs=2))
         res_pool = ctx.enter_context(tc.tile_pool(name="res", bufs=4))
         tanh_pool = ctx.enter_context(tc.tile_pool(name="tanh", bufs=3))
         turn_psum = ctx.enter_context(tc.psum_pool(name="turn", bufs=8 - RING))
@@ -166,7 +165,8 @@ def tile_treelstm_pb_t_kernel(
 
         uT_words = keep.tile([P, 3 * CH], F32, name="uT_words")
         uT = uT_words[:].bitcast(BF16).rearrange("p (n e) -> p n e", e=2)
-        bias_all = keep.tile([P, 2 * BANK], F32, name="bias_all")
+        bias_all = keep.tile([P, BANK], F32, name="bias_all")
+        bias_u = keep.tile([P, U_BLOCKS], F32, name="bias_u")
         w_grouped = keep.tile([P, 12 * CH], BF16, name="w_grouped", align_bytes=64)
         w_codes = keep.tile([P, 3 * CH], U32, name="w_codes", align_bytes=64)
         w_scales = keep.tile([P, 3 * CH], U8, name="w_scales", align_bytes=64)
@@ -182,79 +182,100 @@ def tile_treelstm_pb_t_kernel(
                 out=w_codes[:, c0:c1].bitcast(FP8X4), scales=w_scales[:, c0:c1], in_=w_grouped[:, 4 * c0 : 4 * c1]
             )
 
-        sums, gates_io, gates_u = {}, {}, {}
+        sums, gates_io, gates_u, u_mx = {}, {}, {}, {}
 
-        def tensor_bias(pair):
-            return pair >= FIRST_TENSOR_BIAS
-
-        def tensor_fill(n):
-            pair, k = divmod(n, 6)
-            g, second = divmod(pair, 2)
-            sums[n] = sum_psum.tile([P, BANK], F32, name="sums%d" % n, tag="sum")
-            if k % 3 < 2:
-                parts = [(2 * second + k % 3, 0, BANK, 0)]
-            else:
-                parts = [(2 * second, BANK, 3 * CH, 0), (2 * second + 1, BANK, 3 * CH, CH)]
-            for t, c0, c1, at in parts:
-                dst = sums[n][:, at : at + c1 - c0]
-                if k >= 3:
-                    nc.tensor.matmul_mx(
-                        out=dst,
-                        lhsT=z_codes[g][:, P * t : P * (t + 1)].bitcast(FP8X4),
-                        lhsT_scale=z_scales[g][:, P * t : P * (t + 1)],
-                        rhs=w_codes[:, c0:c1].bitcast(FP8X4),
-                        rhs_scale=w_scales[:, c0:c1],
-                        start=True,
-                        stop=True,
-                    )
-                    continue
-                h_tile = hT[g][:].bitcast(BF16).rearrange("p (t m e) -> p t m e", t=GROUP, m=P, e=2)
-                with_bias = k == 2 and tensor_bias(pair)
+        def tensor_fill(fill):
+            kind, unit, j = fill
+            bank = sum_psum.tile([P, BANK], F32, name="sums_%s_%d_%d" % fill, tag="sum")
+            sums[fill] = bank
+            if kind == "u_mx":
+                c0 = BANK + P * j
+                nc.tensor.matmul_mx(
+                    out=bank[:],
+                    lhsT=w_codes[:, c0 : c0 + P].bitcast(FP8X4),
+                    lhsT_scale=w_scales[:, c0 : c0 + P],
+                    rhs=z_codes[unit][:].bitcast(FP8X4),
+                    rhs_scale=z_scales[unit][:],
+                    start=True,
+                    stop=True,
+                )
+                return
+            g, second = divmod(unit, 2)
+            t = 2 * second + j
+            if kind == "mx":
+                nc.tensor.matmul_mx(
+                    out=bank[:],
+                    lhsT=z_codes[g][:, P * t : P * (t + 1)].bitcast(FP8X4),
+                    lhsT_scale=z_scales[g][:, P * t : P * (t + 1)],
+                    rhs=w_codes[:, 0:BANK].bitcast(FP8X4),
+                    rhs_scale=w_scales[:, 0:BANK],
+                    start=True,
+                    stop=True,
+                )
+                return
+            h_tile = hT[g][:].bitcast(BF16).rearrange("p (t m e) -> p t m e", t=GROUP, m=P, e=2)
+            if kind == "plain":
                 for e in range(2):
                     nc.tensor.matmul(
-                        out=dst,
+                        out=bank[:],
                         lhsT=h_tile[:, t, :, e],
-                        rhs=uT[:, c0:c1, e],
+                        rhs=uT[:, 0:BANK, e],
                         start=(e == 0),
-                        stop=(e == 1 and not with_bias),
+                        stop=(e == 1),
                     )
-                    if k < 2:
-                        ride(pair, 2 * k + e)
-                if with_bias:
-                    nc.tensor.matmul(out=dst, lhsT=ones[:], rhs=bias_rows[:, c0:c1], start=False, stop=True)
+                    ride(unit, 2 * j + e)
+                return
+            for t in (2 * second, 2 * second + 1):
+                c0 = CH * (t % 2)
+                for block in range(U_BLOCKS):
+                    nc.tensor.matmul(
+                        out=bank[:, c0 + P * block : c0 + P * (block + 1)],
+                        lhsT=u_mx[g][:, BANK * block + P * t : BANK * block + P * (t + 1)],
+                        rhs=identity[:],
+                        is_transpose=True,
+                        start=(block == 0),
+                        stop=False,
+                    )
+                for e in range(2):
+                    nc.tensor.matmul(
+                        out=bank[:, c0 : c0 + CH],
+                        lhsT=h_tile[:, t, :, e],
+                        rhs=uT[:, BANK : 3 * CH, e],
+                        start=False,
+                        stop=(e == 1),
+                    )
 
-        def gate_slice(pair, k):
-            g, second = divmod(pair, 2)
+        def empty(fill):
+            kind, unit, j = fill
+            bank = sums[fill]
+            if kind == "u_mx":
+                if j == 0:
+                    u_mx[unit] = u_mx_pool.tile([P, U_BLOCKS * BANK], F32, name="u_mx%d" % unit, tag="u_mx")
+                dst = u_mx[unit][:, BANK * j : BANK * (j + 1)]
+                b_col = bias_u[:, j : j + 1]
+                if j == 0 and unit > 0:
+                    nc.scalar.activation(out=dst, in_=bank[:], func=ACT.Identity, bias=b_col)
+                else:
+                    nc.vector.tensor_scalar(out=dst, in0=bank[:], scalar1=b_col, scalar2=None, op0=ALU.add)
+                return
+            g, second = divmod(unit, 2)
             if g not in gates_io:
                 gates_io[g] = io_pool.tile([P, GROUP * BANK], F32, name="gates_io%d" % g, tag="io")
                 gates_u[g] = u_pool.tile([P, GROUP * CH], F32, name="gates_u%d" % g, tag="u")
-            if k % 3 < 2:
-                t = 2 * second + k % 3
-                return gates_io[g][:, BANK * t : BANK * (t + 1)]
-            return gates_u[g][:, BANK * second : BANK * (second + 1)]
-
-        def vector_empty(n):
-            pair, k = divmod(n, 6)
-            if k == 2 and tensor_bias(pair):
+            if kind == "u":
+                dst = gates_u[g][:, BANK * second : BANK * (second + 1)]
+                nc.scalar.activation(out=dst, in_=bank[:], func=ACT.Tanh)
                 return
-            dst = gate_slice(pair, k)
-            if k >= 3:
-                other = dst
-            else:
-                other = bias_all[:, 0:BANK] if k < 2 else bias_all[:, BANK : 2 * BANK]
-            nc.vector.tensor_tensor(out=dst, in0=sums[n][:], in1=other, op=ALU.add)
-
-        def scalar_empty(pair):
-            nc.scalar.copy(out=gate_slice(pair, 2), in_=sums[6 * pair + 2][:])
+            t = 2 * second + j
+            dst = gates_io[g][:, BANK * t : BANK * (t + 1)]
+            nc.vector.tensor_tensor(
+                out=dst, in0=bank[:], in1=bias_all[:] if kind == "plain" else dst, op=ALU.add
+            )
 
         def sigmoid_io(pair):
             g, second = divmod(pair, 2)
             v = gates_io[g][:, 2 * BANK * second : 2 * BANK * (second + 1)]
             nc.scalar.activation(out=v, in_=v, func=ACT.Sigmoid)
-
-        def tanh_u(pair):
-            v = gate_slice(pair, 2)
-            nc.scalar.activation(out=v, in_=v, func=ACT.Tanh)
 
         res, tanh_c_sb = {}, {}
 
@@ -287,8 +308,6 @@ def tile_treelstm_pb_t_kernel(
 
         def after_pair(pair):
             g, second = divmod(pair, 2)
-            if pair + 1 < PAIRS and tensor_bias(pair + 1):
-                scalar_empty(pair + 1)
             ahead = g + 2
             if not second:
                 if HEAD_GROUPS <= ahead < GROUPS:
@@ -321,64 +340,68 @@ def tile_treelstm_pb_t_kernel(
         nc.vector.tensor_copy(out=uT_words[:, BANK : 3 * CH], in_=u_bank[1][:, 0:CH])
         bias_io = sum_psum.tile([P, BANK], F32, name="bias_io", tag="sum")
         nc.tensor.matmul(out=bias_io[:], lhsT=ones[:], rhs=bias_rows[:, 0:BANK], start=True, stop=True)
-        bias_uu = sum_psum.tile([P, BANK], F32, name="bias_uu", tag="sum")
-        for j in range(2):
+        bias_u_bank = sum_psum.tile([P, BANK], F32, name="bias_u_bank", tag="sum")
+        for block in range(U_BLOCKS):
             nc.tensor.matmul(
-                out=bias_uu[:, CH * j : CH * (j + 1)],
-                lhsT=ones[:],
-                rhs=bias_rows[:, BANK : 3 * CH],
+                out=bias_u_bank[:, block : block + 1],
+                lhsT=bias_rows[:, BANK + P * block : BANK + P * (block + 1)],
+                rhs=ones[:, 0:1],
                 start=True,
                 stop=True,
             )
-        nc.scalar.copy(out=bias_all[:, 0:BANK], in_=bias_io[:])
-        nc.vector.tensor_copy(out=bias_all[:, BANK : 2 * BANK], in_=bias_uu[:])
+        nc.scalar.copy(out=bias_all[:], in_=bias_io[:])
+        nc.vector.tensor_copy(out=bias_u[:], in_=bias_u_bank[:, 0:U_BLOCKS])
 
-        def plain_fill(n):
-            tensor_fill(n)
-            vector_empty(n)
+        def fill_and_empty(fill):
+            tensor_fill(fill)
+            empty(fill)
 
-        plain_fill(0)
+        fill_and_empty(("plain", 0, 0))
         front_w(0)
-        plain_fill(1)
+        fill_and_empty(("plain", 0, 1))
         front_w(1)
         front_z(0, 0)
-        plain_fill(2)
         quantise_w(0, BANK)
         front_w(2)
         quantise_z(0, 0, 1)
-        plain_fill(6)
+        fill_and_empty(("plain", 1, 0))
         quantise_w(BANK, 3 * CH)
         front_z(0, 1)
-        plain_fill(7)
+        fill_and_empty(("plain", 1, 1))
         quantise_z(0, 1, 2)
-        plain_fill(8)
         front_h(1)
         front_z(1, 0)
         front_z(1, 1)
-        for n in (3, 4, 5):
-            tensor_fill(n)
-        for n in (3, 4, 5):
-            vector_empty(n)
+        first_mx = [("mx", 0, 0), ("mx", 0, 1), ("u_mx", 0, 0), ("u_mx", 0, 1)]
+        for fill in first_mx:
+            tensor_fill(fill)
+        for fill in first_mx:
+            empty(fill)
         quantise_z(1)
         front_z(2, 0)
         front_z(2, 1)
         front_h(2)
         sigmoid_io(0)
-        tanh_u(0)
+        fill_and_empty(("u", 0, 0))
         after_pair(0)
 
-        for n in range(HEAD_FILLS, FILLS + LEAD):
-            if n < FILLS:
-                tensor_fill(n)
-            if n - LEAD < HEAD_FILLS:
+        fills = []
+        for pair in range(PAIRS):
+            g, second = divmod(pair, 2)
+            of_pair = [("plain", pair, 0), ("plain", pair, 1), ("u", pair, 0), ("mx", pair, 0), ("mx", pair, 1)]
+            if not second and g + 1 < GROUPS:
+                of_pair += [("u_mx", g + 1, block) for block in range(U_BLOCKS)]
+            fills += [fill for fill in of_pair if fill not in sums]
+        for n in range(len(fills) + LEAD):
+            if n < len(fills):
+                tensor_fill(fills[n])
+            if n < LEAD:
                 continue
-            pair, k = divmod(n - LEAD, 6)
-            vector_empty(n - LEAD)
-            if k == 4:
-                sigmoid_io(pair)
-            if k == 5:
-                tanh_u(pair)
-                after_pair(pair)
+            kind, unit, j = fills[n - LEAD]
+            empty(fills[n - LEAD])
+            if kind == "mx" and j == 1:
+                sigmoid_io(unit)
+                after_pair(unit)
 
         last = GROUPS - 1
         for t0 in (0, 2):

@@ -20,8 +20,8 @@ GROUPS = TILES // GROUP
 PAIRS = TILES // 2
 BANK = 512
 U_BLOCKS = CH // P
-RING = 5
-LEAD = RING - 1
+V_RING = 4
+S_RING = 4
 HEAD_GROUPS = 3
 GPSIMD_H = 2
 FLOPS = 2 * NODES * (SIZE + CH) * 3 * CH
@@ -40,8 +40,8 @@ def tile_treelstm_pb_t_kernel(
         u_mx_pool = ctx.enter_context(tc.tile_pool(name="u_mx", bufs=2))
         res_pool = ctx.enter_context(tc.tile_pool(name="res", bufs=4))
         tanh_pool = ctx.enter_context(tc.tile_pool(name="tanh", bufs=3))
-        turn_psum = ctx.enter_context(tc.psum_pool(name="turn", bufs=8 - RING))
-        sum_psum = ctx.enter_context(tc.psum_pool(name="sums", bufs=RING))
+        v_psum = ctx.enter_context(tc.psum_pool(name="v_ring", bufs=V_RING))
+        s_psum = ctx.enter_context(tc.psum_pool(name="s_ring", bufs=S_RING))
 
         z_dram = z0.rearrange("(p t) k -> p t k", t=TILES)
         h_dram = h_tilde.rearrange("(p t) k -> p t k", t=TILES)
@@ -105,16 +105,22 @@ def tile_treelstm_pb_t_kernel(
                 bank[:, P * (at % 4) : P * (at % 4 + 1)], src_words[:, w0 : w0 + 2 * P - 1 : 2], identity[:]
             )
 
+        def v_bank(name):
+            return v_psum.tile([P, BANK], F32, name=name, tag="v")
+
+        def s_bank(name):
+            return s_psum.tile([P, BANK], F32, name=name, tag="s")
+
         h_bank, z_bank = {}, {}
 
         def turn_h(g, j):
             if j == 0:
-                h_bank[g] = turn_psum.tile([P, BANK], F32, name="h_bank%d" % g, tag="turn")
+                h_bank[g] = s_bank("h_bank%d" % g)
             turn(h_bank[g], j, words(h_in[g]), j)
 
         def turn_z(g, half, j):
             if j == 0:
-                z_bank[g, half] = turn_psum.tile([P, BANK], F32, name="z_bank%d_%d" % (g, half), tag="turn")
+                z_bank[g, half] = s_bank("z_bank%d_%d" % (g, half))
             turn_mx(z_bank[g, half], 4 * half + j, words(z_in[g]))
 
         def regroup(dst_words, bank):
@@ -172,7 +178,7 @@ def tile_treelstm_pb_t_kernel(
         w_scales = keep.tile([P, 3 * CH], U8, name="w_scales", align_bytes=64)
 
         def front_w(j):
-            bank = sum_psum.tile([P, BANK], F32, name="w_bank%d" % j, tag="sum")
+            bank = s_bank("w_bank%d" % j)
             for square in range(4):
                 turn_mx(bank, square, words(w_in[j]))
             regroup(w_grouped[:].bitcast(F32)[:, BANK * j : BANK * (j + 1)], bank)
@@ -184,9 +190,13 @@ def tile_treelstm_pb_t_kernel(
 
         sums, gates_io, gates_u, u_mx = {}, {}, {}, {}
 
+        def on_scalar(fill):
+            kind, unit, j = fill
+            return kind == "u" or (kind == "u_mx" and j == 0)
+
         def tensor_fill(fill):
             kind, unit, j = fill
-            bank = sum_psum.tile([P, BANK], F32, name="sums_%s_%d_%d" % fill, tag="sum")
+            bank = (s_bank if on_scalar(fill) else v_bank)("sums_%s_%d_%d" % fill)
             sums[fill] = bank
             if kind == "u_mx":
                 c0 = BANK + P * j
@@ -253,7 +263,7 @@ def tile_treelstm_pb_t_kernel(
                     u_mx[unit] = u_mx_pool.tile([P, U_BLOCKS * BANK], F32, name="u_mx%d" % unit, tag="u_mx")
                 dst = u_mx[unit][:, BANK * j : BANK * (j + 1)]
                 b_col = bias_u[:, j : j + 1]
-                if j == 0 and unit > 0:
+                if on_scalar(fill):
                     nc.scalar.activation(out=dst, in_=bank[:], func=ACT.Identity, bias=b_col)
                 else:
                     nc.vector.tensor_scalar(out=dst, in0=bank[:], scalar1=b_col, scalar2=None, op0=ALU.add)
@@ -306,30 +316,7 @@ def tile_treelstm_pb_t_kernel(
                 out=out_dram[:, GROUP * g + t0 : GROUP * g + t1, c0:c1], in_=res[g][:, t0:t1, c0:c1]
             )
 
-        def after_pair(pair):
-            g, second = divmod(pair, 2)
-            ahead = g + 2
-            if not second:
-                if HEAD_GROUPS <= ahead < GROUPS:
-                    regroup_z(ahead, 1)
-                return
-            if HEAD_GROUPS <= ahead < GROUPS:
-                copy_h(ahead)
-            if HEAD_GROUPS <= ahead + 1 < GROUPS:
-                regroup_z(ahead + 1, 0)
-            if g < GROUPS - 1:
-                cell(nc.gpsimd, g, 0, GROUP)
-            if g >= 1:
-                tanh_c(g - 1, 0, GROUP)
-                if g < GROUPS - 1:
-                    hidden(nc.gpsimd, g - 1, 0, GPSIMD_H)
-            if ahead < GROUPS:
-                quantise_z(ahead)
-            if g >= 2:
-                hidden(nc.vector, g - 2, GPSIMD_H, GROUP)
-                store(g - 2, 0, GROUP, 0, CH)
-
-        u_bank = [sum_psum.tile([P, BANK], F32, name="u_bank%d" % j, tag="sum") for j in range(2)]
+        u_bank = [v_bank("u_bank%d" % j) for j in range(2)]
         for j in range(2):
             for b in range(2):
                 turn(u_bank[0], 2 * j + b, words(u_in[j]), b)
@@ -338,9 +325,9 @@ def tile_treelstm_pb_t_kernel(
         for b in range(2):
             turn(u_bank[1], b, words(u_in[2]), b)
         nc.vector.tensor_copy(out=uT_words[:, BANK : 3 * CH], in_=u_bank[1][:, 0:CH])
-        bias_io = sum_psum.tile([P, BANK], F32, name="bias_io", tag="sum")
+        bias_io = s_bank("bias_io")
         nc.tensor.matmul(out=bias_io[:], lhsT=ones[:], rhs=bias_rows[:, 0:BANK], start=True, stop=True)
-        bias_u_bank = sum_psum.tile([P, BANK], F32, name="bias_u_bank", tag="sum")
+        bias_u_bank = v_bank("bias_u_bank")
         for block in range(U_BLOCKS):
             nc.tensor.matmul(
                 out=bias_u_bank[:, block : block + 1],
@@ -352,9 +339,11 @@ def tile_treelstm_pb_t_kernel(
         nc.scalar.copy(out=bias_all[:], in_=bias_io[:])
         nc.vector.tensor_copy(out=bias_u[:], in_=bias_u_bank[:, 0:U_BLOCKS])
 
-        def fill_and_empty(fill):
-            tensor_fill(fill)
-            empty(fill)
+        def fill_and_empty(*fills):
+            for fill in fills:
+                tensor_fill(fill)
+            for fill in fills:
+                empty(fill)
 
         fill_and_empty(("plain", 0, 0))
         front_w(0)
@@ -369,39 +358,51 @@ def tile_treelstm_pb_t_kernel(
         front_z(0, 1)
         fill_and_empty(("plain", 1, 1))
         quantise_z(0, 1, 2)
-        front_h(1)
+        fill_and_empty(("mx", 0, 0), ("mx", 0, 1))
+        fill_and_empty(("u_mx", 0, 0), ("u_mx", 0, 1))
         front_z(1, 0)
         front_z(1, 1)
-        first_mx = [("mx", 0, 0), ("mx", 0, 1), ("u_mx", 0, 0), ("u_mx", 0, 1)]
-        for fill in first_mx:
-            tensor_fill(fill)
-        for fill in first_mx:
-            empty(fill)
         quantise_z(1)
-        front_z(2, 0)
-        front_z(2, 1)
-        front_h(2)
-        sigmoid_io(0)
-        fill_and_empty(("u", 0, 0))
-        after_pair(0)
+        front_h(1)
 
-        fills = []
         for pair in range(PAIRS):
             g, second = divmod(pair, 2)
-            of_pair = [("plain", pair, 0), ("plain", pair, 1), ("u", pair, 0), ("mx", pair, 0), ("mx", pair, 1)]
+            ahead = g + 2
+            for j in range(2):
+                if ("plain", pair, j) not in sums:
+                    tensor_fill(("plain", pair, j))
+            if ahead == 2:
+                front_z(ahead, second)
+                if second:
+                    front_h(ahead)
+            elif ahead < GROUPS:
+                regroup_z(ahead, second)
+                if second:
+                    copy_h(ahead)
+            fill_and_empty(("u", pair, 0))
+            if pair > 0:
+                for j in range(2):
+                    tensor_fill(("mx", pair, j))
+                for kind in ("plain", "mx"):
+                    for j in range(2):
+                        if (kind, pair, j) != ("plain", 1, 0) and (kind, pair, j) != ("plain", 1, 1):
+                            empty((kind, pair, j))
             if not second and g + 1 < GROUPS:
-                of_pair += [("u_mx", g + 1, block) for block in range(U_BLOCKS)]
-            fills += [fill for fill in of_pair if fill not in sums]
-        for n in range(len(fills) + LEAD):
-            if n < len(fills):
-                tensor_fill(fills[n])
-            if n < LEAD:
+                fill_and_empty(("u_mx", g + 1, 0), ("u_mx", g + 1, 1))
+            sigmoid_io(pair)
+            if not second:
                 continue
-            kind, unit, j = fills[n - LEAD]
-            empty(fills[n - LEAD])
-            if kind == "mx" and j == 1:
-                sigmoid_io(unit)
-                after_pair(unit)
+            if g < GROUPS - 1:
+                cell(nc.gpsimd, g, 0, GROUP)
+            if g >= 1:
+                tanh_c(g - 1, 0, GROUP)
+                if g < GROUPS - 1:
+                    hidden(nc.gpsimd, g - 1, 0, GPSIMD_H)
+            if ahead < GROUPS:
+                quantise_z(ahead)
+            if g >= 2:
+                hidden(nc.vector, g - 2, GPSIMD_H, GROUP)
+                store(g - 2, 0, GROUP, 0, CH)
 
         last = GROUPS - 1
         for t0 in (0, 2):

@@ -23,7 +23,6 @@ U_BLOCKS = CH // P
 V_RING = 4
 S_RING = 4
 HEAD_GROUPS = 3
-GPSIMD_H = 2
 FLOPS = 2 * NODES * (SIZE + CH) * 3 * CH
 
 
@@ -396,12 +395,10 @@ def tile_treelstm_pb_t_kernel(
                 cell(nc.gpsimd, g, 0, GROUP)
             if g >= 1:
                 tanh_c(g - 1, 0, GROUP)
-                if g < GROUPS - 1:
-                    hidden(nc.gpsimd, g - 1, 0, GPSIMD_H)
             if ahead < GROUPS:
                 quantise_z(ahead)
             if g >= 2:
-                hidden(nc.vector, g - 2, GPSIMD_H, GROUP)
+                hidden(nc.vector, g - 2, 0, GROUP)
                 store(g - 2, 0, GROUP, 0, CH)
 
         last = GROUPS - 1

@@ -161,13 +161,6 @@ def tile_treelstm_pb_t_kernel(
                 turn_z(g, half, j)
             regroup_z(g, half)
 
-        def ride(pair, j):
-            g = pair // 2 + 2
-            if HEAD_GROUPS <= g < GROUPS:
-                turn_z(g, pair % 2, j)
-                if pair % 2 == 1:
-                    turn_h(g, j)
-
         uT_words = keep.tile([P, 3 * CH], F32, name="uT_words")
         uT = uT_words[:].bitcast(BF16).rearrange("p (n e) -> p n e", e=2)
         bias_all = keep.tile([P, BANK], F32, name="bias_all")
@@ -232,26 +225,26 @@ def tile_treelstm_pb_t_kernel(
                         start=(e == 0),
                         stop=(e == 1),
                     )
-                    ride(unit, 2 * j + e)
                 return
             for t in (2 * second, 2 * second + 1):
-                c0 = CH * (t % 2)
                 for block in range(U_BLOCKS):
+                    c0 = CH * (t % 2) + P * block
                     nc.tensor.matmul(
-                        out=bank[:, c0 + P * block : c0 + P * (block + 1)],
+                        out=bank[:, c0 : c0 + P],
                         lhsT=u_mx[g][:, BANK * block + P * t : BANK * block + P * (t + 1)],
                         rhs=identity[:],
                         is_transpose=True,
-                        start=(block == 0),
+                        start=(c0 == 0),
                         stop=False,
                     )
+            for t in (2 * second, 2 * second + 1):
                 for e in range(2):
                     nc.tensor.matmul(
-                        out=bank[:, c0 : c0 + CH],
+                        out=bank[:, CH * (t % 2) : CH * (t % 2 + 1)],
                         lhsT=h_tile[:, t, :, e],
                         rhs=uT[:, BANK : 3 * CH, e],
                         start=False,
-                        stop=(e == 1),
+                        stop=(t % 2 == 1 and e == 1),
                     )
 
         def empty(fill):
@@ -370,14 +363,10 @@ def tile_treelstm_pb_t_kernel(
             for j in range(2):
                 if ("plain", pair, j) not in sums:
                     tensor_fill(("plain", pair, j))
-            if ahead == 2:
+            if ahead < GROUPS:
                 front_z(ahead, second)
                 if second:
                     front_h(ahead)
-            elif ahead < GROUPS:
-                regroup_z(ahead, second)
-                if second:
-                    copy_h(ahead)
             fill_and_empty(("u", pair, 0))
             if pair > 0:
                 for j in range(2):

@@ -22,6 +22,7 @@ BANK = 512
 U_BLOCKS = CH // P
 V_RING = 4
 S_RING = 4
+WARM_UP = 4
 HEAD_GROUPS = 3
 FLOPS = 2 * NODES * (SIZE + CH) * 3 * CH
 
@@ -47,6 +48,8 @@ def tile_treelstm_pb_t_kernel(
         fc_dram = fc_sum.rearrange("(p t) k -> p t k", t=TILES)
         out_dram = out.rearrange("(p t) c -> p t c", t=TILES)
 
+        ones = keep.tile([P, BANK], BF16, name="ones")
+        nc.vector.memset(ones[:], 1.0)
         bias_rows = keep.tile([P, 3 * CH], BF16, name="bias_rows")
         nc.vector.memset(bias_rows[:].bitcast(I32), 0)
         for j, b in enumerate((b_i, b_o, b_u)):
@@ -55,8 +58,6 @@ def tile_treelstm_pb_t_kernel(
             )
         identity = keep.tile([P, P], F32, name="identity")
         make_identity(nc, identity[:])
-        ones = keep.tile([P, P], BF16, name="ones")
-        nc.vector.memset(ones[:], 1.0)
         warm = keep.tile([P, 8], F32, name="warm")
         nc.vector.memset(warm[:], 0.0)
         nc.scalar.activation(out=warm[:], in_=warm[:], func=ACT.Sigmoid)
@@ -184,7 +185,7 @@ def tile_treelstm_pb_t_kernel(
 
         def on_scalar(fill):
             kind, unit, j = fill
-            return kind == "u" or (kind == "u_mx" and j == 0)
+            return kind in ("u", "u_mx")
 
         def tensor_fill(fill):
             kind, unit, j = fill
@@ -308,6 +309,9 @@ def tile_treelstm_pb_t_kernel(
                 out=out_dram[:, GROUP * g + t0 : GROUP * g + t1, c0:c1], in_=res[g][:, t0:t1, c0:c1]
             )
 
+        warm_bank = v_bank("warm_bank")
+        for n in range(WARM_UP):
+            nc.tensor.matmul(out=warm_bank[:], lhsT=ones[:, 0:P], rhs=ones[:], start=True, stop=True)
         u_bank = [v_bank("u_bank%d" % j) for j in range(2)]
         for j in range(2):
             for b in range(2):
@@ -318,7 +322,7 @@ def tile_treelstm_pb_t_kernel(
             turn(u_bank[1], b, words(u_in[2]), b)
         nc.vector.tensor_copy(out=uT_words[:, BANK : 3 * CH], in_=u_bank[1][:, 0:CH])
         bias_io = s_bank("bias_io")
-        nc.tensor.matmul(out=bias_io[:], lhsT=ones[:], rhs=bias_rows[:, 0:BANK], start=True, stop=True)
+        nc.tensor.matmul(out=bias_io[:], lhsT=ones[:, 0:P], rhs=bias_rows[:, 0:BANK], start=True, stop=True)
         bias_u_bank = v_bank("bias_u_bank")
         for block in range(U_BLOCKS):
             nc.tensor.matmul(

@@ -129,6 +129,9 @@ def tile_treelstm_pb_t_kernel(
                 in_=bank[:].rearrange("p (s v m) -> p s m v", s=2, v=2, m=P),
             )
 
+        def halves(bank_words):
+            return bank_words.bitcast(BF16).rearrange("p (n e) -> p e n", e=2)
+
         hT, z_grouped, z_codes, z_scales = {}, {}, {}, {}
 
         def copy_h(g):
@@ -162,8 +165,7 @@ def tile_treelstm_pb_t_kernel(
                 turn_z(g, half, j)
             regroup_z(g, half)
 
-        uT_words = keep.tile([P, 3 * CH], F32, name="uT_words")
-        uT = uT_words[:].bitcast(BF16).rearrange("p (n e) -> p n e", e=2)
+        uT = keep.tile([P, 2, 3 * CH], BF16, name="uT")
         bias_all = keep.tile([P, BANK], F32, name="bias_all")
         bias_u = keep.tile([P, U_BLOCKS], F32, name="bias_u")
         w_grouped = keep.tile([P, 12 * CH], BF16, name="w_grouped", align_bytes=64)
@@ -222,7 +224,7 @@ def tile_treelstm_pb_t_kernel(
                     nc.tensor.matmul(
                         out=bank[:],
                         lhsT=h_tile[:, t, :, e],
-                        rhs=uT[:, 0:BANK, e],
+                        rhs=uT[:, e, 0:BANK],
                         start=(e == 0),
                         stop=(e == 1),
                     )
@@ -243,7 +245,7 @@ def tile_treelstm_pb_t_kernel(
                     nc.tensor.matmul(
                         out=bank[:, CH * (t % 2) : CH * (t % 2 + 1)],
                         lhsT=h_tile[:, t, :, e],
-                        rhs=uT[:, BANK : 3 * CH, e],
+                        rhs=uT[:, e, BANK : 3 * CH],
                         start=False,
                         stop=(t % 2 == 1 and e == 1),
                     )
@@ -316,11 +318,11 @@ def tile_treelstm_pb_t_kernel(
         for j in range(2):
             for b in range(2):
                 turn(u_bank[0], 2 * j + b, words(u_in[j]), b)
-        nc.vector.tensor_copy(out=uT_words[:, 0:BANK], in_=u_bank[0][:])
+        nc.vector.tensor_copy(out=uT[:, :, 0:BANK], in_=halves(u_bank[0][:]))
         front_h(0)
         for b in range(2):
             turn(u_bank[1], b, words(u_in[2]), b)
-        nc.vector.tensor_copy(out=uT_words[:, BANK : 3 * CH], in_=u_bank[1][:, 0:CH])
+        nc.vector.tensor_copy(out=uT[:, :, BANK : 3 * CH], in_=halves(u_bank[1][:, 0:CH]))
         bias_io = s_bank("bias_io")
         nc.tensor.matmul(out=bias_io[:], lhsT=ones[:, 0:P], rhs=bias_rows[:, 0:BANK], start=True, stop=True)
         bias_u_bank = v_bank("bias_u_bank")

@@ -19,9 +19,19 @@ GROUP = 4
 GROUPS = TILES // GROUP
 PAIRS = TILES // 2
 BANK = 512
-U_BLOCKS = CH // P
+BLOCKS = 3 * CH // P
+IO_BLOCKS = range(0, 4)
+U_BLOCKS = range(4, BLOCKS)
+WHOLE_GROUPS = (GROUPS - 1,)
 V_RING = 4
 S_RING = 4
+IO_AT = 1
+DIRECT_U = (0, 1)
+GPSIMD_H = 1
+V5 = True
+IO_SCALAR = (0, 2)
+GPSIMD_GROUPS = 6
+U_FIRST = True
 WARM_UP = 4
 HEAD_GROUPS = 3
 FLOPS = 2 * NODES * (SIZE + CH) * 3 * CH
@@ -38,6 +48,7 @@ def tile_treelstm_pb_t_kernel(
         io_pool = ctx.enter_context(tc.tile_pool(name="io", bufs=4))
         u_pool = ctx.enter_context(tc.tile_pool(name="u", bufs=3))
         u_mx_pool = ctx.enter_context(tc.tile_pool(name="u_mx", bufs=2))
+        io_mx_pool = ctx.enter_context(tc.tile_pool(name="io_mx", bufs=1))
         res_pool = ctx.enter_context(tc.tile_pool(name="res", bufs=4))
         tanh_pool = ctx.enter_context(tc.tile_pool(name="tanh", bufs=3))
         v_psum = ctx.enter_context(tc.psum_pool(name="v_ring", bufs=V_RING))
@@ -167,7 +178,8 @@ def tile_treelstm_pb_t_kernel(
 
         uT = keep.tile([P, 2, 3 * CH], BF16, name="uT")
         bias_all = keep.tile([P, BANK], F32, name="bias_all")
-        bias_u = keep.tile([P, U_BLOCKS], F32, name="bias_u")
+        bias_uu = keep.tile([P, BANK], F32, name="bias_uu")
+        bias_cols = keep.tile([P, BLOCKS], F32, name="bias_cols")
         w_grouped = keep.tile([P, 12 * CH], BF16, name="w_grouped", align_bytes=64)
         w_codes = keep.tile([P, 3 * CH], U32, name="w_codes", align_bytes=64)
         w_scales = keep.tile([P, 3 * CH], U8, name="w_scales", align_bytes=64)
@@ -183,18 +195,28 @@ def tile_treelstm_pb_t_kernel(
                 out=w_codes[:, c0:c1].bitcast(FP8X4), scales=w_scales[:, c0:c1], in_=w_grouped[:, 4 * c0 : 4 * c1]
             )
 
-        sums, gates_io, gates_u, u_mx = {}, {}, {}, {}
+        sums, gates_io, gates_u, col_mx = {}, {}, {}, {}
 
-        def on_scalar(fill):
+        def leaves_by_scalar(fill):
             kind, unit, j = fill
-            return kind in ("u", "u_mx")
+            return kind in ("u", "whole") or (kind == "col_mx" and j in IO_SCALAR + ((4,) if V5 else (4, 5)))
+
+        def turned_block(bank, at, g, t, block, start):
+            nc.tensor.matmul(
+                out=bank[:, at : at + P],
+                lhsT=col_mx[g, block][:, P * t : P * (t + 1)],
+                rhs=identity[:],
+                is_transpose=True,
+                start=start,
+                stop=False,
+            )
 
         def tensor_fill(fill):
             kind, unit, j = fill
-            bank = (s_bank if on_scalar(fill) else v_bank)("sums_%s_%d_%d" % fill)
+            bank = (s_bank if leaves_by_scalar(fill) else v_bank)("sums_%s_%d_%d" % fill)
             sums[fill] = bank
-            if kind == "u_mx":
-                c0 = BANK + P * j
+            if kind == "col_mx":
+                c0 = P * j
                 nc.tensor.matmul_mx(
                     out=bank[:],
                     lhsT=w_codes[:, c0 : c0 + P].bitcast(FP8X4),
@@ -219,46 +241,60 @@ def tile_treelstm_pb_t_kernel(
                 )
                 return
             h_tile = hT[g][:].bitcast(BF16).rearrange("p (t m e) -> p t m e", t=GROUP, m=P, e=2)
-            if kind == "plain":
+            if kind == "mx_u":
+                for t in (2 * second, 2 * second + 1):
+                    nc.tensor.matmul_mx(
+                        out=bank[:, CH * (t % 2) : CH * (t % 2 + 1)],
+                        lhsT=z_codes[g][:, P * t : P * (t + 1)].bitcast(FP8X4),
+                        lhsT_scale=z_scales[g][:, P * t : P * (t + 1)],
+                        rhs=w_codes[:, BANK : 3 * CH].bitcast(FP8X4),
+                        rhs_scale=w_scales[:, BANK : 3 * CH],
+                        start=True,
+                        stop=True,
+                    )
+                return
+            if kind in ("plain", "whole"):
+                if kind == "whole":
+                    for block in IO_BLOCKS:
+                        turned_block(bank, P * block, g, t, block, block == 0)
                 for e in range(2):
                     nc.tensor.matmul(
                         out=bank[:],
                         lhsT=h_tile[:, t, :, e],
                         rhs=uT[:, e, 0:BANK],
-                        start=(e == 0),
+                        start=(kind == "plain" and e == 0),
                         stop=(e == 1),
                     )
                 return
-            for t in (2 * second, 2 * second + 1):
-                for block in range(U_BLOCKS):
-                    c0 = CH * (t % 2) + P * block
-                    nc.tensor.matmul(
-                        out=bank[:, c0 : c0 + P],
-                        lhsT=u_mx[g][:, BANK * block + P * t : BANK * block + P * (t + 1)],
-                        rhs=identity[:],
-                        is_transpose=True,
-                        start=(c0 == 0),
-                        stop=False,
-                    )
+            for t in (2 * second, 2 * second + 1) if kind == "u" else ():
+                for block in U_BLOCKS:
+                    at = CH * (t % 2) + P * (block % 2)
+                    turned_block(bank, at, g, t, block, at == 0)
             for t in (2 * second, 2 * second + 1):
                 for e in range(2):
                     nc.tensor.matmul(
                         out=bank[:, CH * (t % 2) : CH * (t % 2 + 1)],
                         lhsT=h_tile[:, t, :, e],
                         rhs=uT[:, e, BANK : 3 * CH],
-                        start=False,
-                        stop=(t % 2 == 1 and e == 1),
+                        start=(kind == "plain_u" and e == 0),
+                        stop=(e == 1 and (kind == "plain_u" or t % 2 == 1)),
                     )
 
         def empty(fill):
             kind, unit, j = fill
             bank = sums[fill]
-            if kind == "u_mx":
+            if kind == "col_mx":
                 if j == 0:
-                    u_mx[unit] = u_mx_pool.tile([P, U_BLOCKS * BANK], F32, name="u_mx%d" % unit, tag="u_mx")
-                dst = u_mx[unit][:, BANK * j : BANK * (j + 1)]
-                b_col = bias_u[:, j : j + 1]
-                if on_scalar(fill):
+                    io_mx = io_mx_pool.tile([P, len(IO_BLOCKS) * BANK], F32, name="io_mx%d" % unit, tag="io_mx")
+                    for block in IO_BLOCKS:
+                        col_mx[unit, block] = io_mx[:, BANK * block : BANK * (block + 1)]
+                if j == 4:
+                    u_mx = u_mx_pool.tile([P, len(U_BLOCKS) * BANK], F32, name="u_mx%d" % unit, tag="u_mx")
+                    for block in U_BLOCKS:
+                        col_mx[unit, block] = u_mx[:, BANK * (block - 4) : BANK * (block - 3)]
+                dst = col_mx[unit, j]
+                b_col = bias_cols[:, j : j + 1]
+                if leaves_by_scalar(fill):
                     nc.scalar.activation(out=dst, in_=bank[:], func=ACT.Identity, bias=b_col)
                 else:
                     nc.vector.tensor_scalar(out=dst, in0=bank[:], scalar1=b_col, scalar2=None, op0=ALU.add)
@@ -271,11 +307,25 @@ def tile_treelstm_pb_t_kernel(
                 dst = gates_u[g][:, BANK * second : BANK * (second + 1)]
                 nc.scalar.activation(out=dst, in_=bank[:], func=ACT.Tanh)
                 return
+            if kind in ("plain_u", "mx_u"):
+                dst = gates_u[g][:, BANK * second : BANK * (second + 1)]
+                nc.vector.tensor_tensor(
+                    out=dst, in0=bank[:], in1=bias_uu[:] if kind == "plain_u" else dst, op=ALU.add
+                )
+                return
             t = 2 * second + j
             dst = gates_io[g][:, BANK * t : BANK * (t + 1)]
+            if kind == "whole":
+                nc.scalar.activation(out=dst, in_=bank[:], func=ACT.Sigmoid)
+                return
             nc.vector.tensor_tensor(
                 out=dst, in0=bank[:], in1=bias_all[:] if kind == "plain" else dst, op=ALU.add
             )
+
+        def tanh_u(pair):
+            g, second = divmod(pair, 2)
+            v = gates_u[g][:, BANK * second : BANK * (second + 1)]
+            nc.scalar.activation(out=v, in_=v, func=ACT.Tanh)
 
         def sigmoid_io(pair):
             g, second = divmod(pair, 2)
@@ -325,17 +375,27 @@ def tile_treelstm_pb_t_kernel(
         nc.vector.tensor_copy(out=uT[:, :, BANK : 3 * CH], in_=halves(u_bank[1][:, 0:CH]))
         bias_io = s_bank("bias_io")
         nc.tensor.matmul(out=bias_io[:], lhsT=ones[:, 0:P], rhs=bias_rows[:, 0:BANK], start=True, stop=True)
-        bias_u_bank = v_bank("bias_u_bank")
-        for block in range(U_BLOCKS):
+        bias_cols_bank = v_bank("bias_cols_bank")
+        for block in range(BLOCKS):
             nc.tensor.matmul(
-                out=bias_u_bank[:, block : block + 1],
-                lhsT=bias_rows[:, BANK + P * block : BANK + P * (block + 1)],
+                out=bias_cols_bank[:, block : block + 1],
+                lhsT=bias_rows[:, P * block : P * (block + 1)],
                 rhs=ones[:, 0:1],
                 start=True,
                 stop=True,
             )
+        bias_u_bank = v_bank("bias_u_bank")
+        for j in range(2):
+            nc.tensor.matmul(
+                out=bias_u_bank[:, CH * j : CH * (j + 1)],
+                lhsT=ones[:, 0:P],
+                rhs=bias_rows[:, BANK : 3 * CH],
+                start=True,
+                stop=True,
+            )
         nc.scalar.copy(out=bias_all[:], in_=bias_io[:])
-        nc.vector.tensor_copy(out=bias_u[:], in_=bias_u_bank[:, 0:U_BLOCKS])
+        nc.vector.tensor_copy(out=bias_cols[:], in_=bias_cols_bank[:, 0:BLOCKS])
+        nc.vector.tensor_copy(out=bias_uu[:], in_=bias_u_bank[:])
 
         def fill_and_empty(*fills):
             for fill in fills:
@@ -348,6 +408,7 @@ def tile_treelstm_pb_t_kernel(
         fill_and_empty(("plain", 0, 1))
         front_w(1)
         front_z(0, 0)
+        fill_and_empty(("plain_u", 0, 0))
         quantise_w(0, BANK)
         front_w(2)
         quantise_z(0, 0, 1)
@@ -356,44 +417,79 @@ def tile_treelstm_pb_t_kernel(
         front_z(0, 1)
         fill_and_empty(("plain", 1, 1))
         quantise_z(0, 1, 2)
-        fill_and_empty(("mx", 0, 0), ("mx", 0, 1))
-        fill_and_empty(("u_mx", 0, 0), ("u_mx", 0, 1))
         front_z(1, 0)
-        front_z(1, 1)
-        quantise_z(1)
+        fill_and_empty(("mx", 0, 0), ("mx", 0, 1), ("mx_u", 0, 0))
         front_h(1)
+        front_z(1, 1)
+        fill_and_empty(("plain_u", 1, 0))
+        fill_and_empty(("mx", 1, 0), ("mx", 1, 1), ("mx_u", 1, 0))
+        quantise_z(1)
+        sigmoid_io(0)
+        tanh_u(0)
+        front_z(2, 0)
+        sigmoid_io(1)
+        tanh_u(1)
+        front_z(2, 1)
+        front_h(2)
 
-        for pair in range(PAIRS):
+        for pair in range(1, PAIRS):
             g, second = divmod(pair, 2)
             ahead = g + 2
-            for j in range(2):
-                if ("plain", pair, j) not in sums:
-                    tensor_fill(("plain", pair, j))
-            if ahead < GROUPS:
-                front_z(ahead, second)
-                if second:
-                    front_h(ahead)
-            fill_and_empty(("u", pair, 0))
-            if pair > 0:
+            whole = g in WHOLE_GROUPS
+            direct_u = g in DIRECT_U
+            if pair > 1:
+                if whole:
+                    fill_and_empty(("u", pair, 0))
                 for j in range(2):
-                    tensor_fill(("mx", pair, j))
-                for kind in ("plain", "mx"):
+                    if whole:
+                        fill_and_empty(("whole", pair, j))
+                    else:
+                        tensor_fill(("plain", pair, j))
+                if direct_u:
+                    tensor_fill(("plain_u", pair, 0))
+                if ahead < GROUPS:
+                    front_z(ahead, second)
+                    if second:
+                        front_h(ahead)
+                if not whole and not direct_u:
+                    fill_and_empty(("u", pair, 0))
+                if not whole:
                     for j in range(2):
-                        if (kind, pair, j) != ("plain", 1, 0) and (kind, pair, j) != ("plain", 1, 1):
-                            empty((kind, pair, j))
-            if not second and g + 1 < GROUPS:
-                fill_and_empty(("u_mx", g + 1, 0), ("u_mx", g + 1, 1))
-            sigmoid_io(pair)
+                        empty(("plain", pair, j))
+                    tensor_fill(("mx", pair, 0))
+                    if direct_u:
+                        empty(("plain_u", pair, 0))
+                    tensor_fill(("mx", pair, 1))
+                    if pair == 2:
+                        quantise_z(2)
+                    empty(("mx", pair, 0))
+                    if direct_u:
+                        tensor_fill(("mx_u", pair, 0))
+                    empty(("mx", pair, 1))
+                    if direct_u:
+                        empty(("mx_u", pair, 0))
+                if not second and g + 1 < GROUPS and g + 1 not in DIRECT_U:
+                    fill_and_empty(("col_mx", g + 1, 4), ("col_mx", g + 1, 5))
+                if second == IO_AT and g + 1 in WHOLE_GROUPS:
+                    fill_and_empty(*[("col_mx", g + 1, block) for block in IO_BLOCKS])
+                if not whole:
+                    sigmoid_io(pair)
+                    if direct_u:
+                        tanh_u(pair)
+            if g == GPSIMD_GROUPS and g < GROUPS - 1:
+                cell(nc.vector if second else nc.gpsimd, g, 2 * second, 2 * second + 2)
             if not second:
                 continue
-            if g < GROUPS - 1:
+            if g < GPSIMD_GROUPS:
                 cell(nc.gpsimd, g, 0, GROUP)
             if g >= 1:
                 tanh_c(g - 1, 0, GROUP)
-            if ahead < GROUPS:
+                if g < GPSIMD_GROUPS and GPSIMD_H:
+                    hidden(nc.gpsimd, g - 1, 0, GPSIMD_H)
+            if 2 < ahead < GROUPS:
                 quantise_z(ahead)
             if g >= 2:
-                hidden(nc.vector, g - 2, 0, GROUP)
+                hidden(nc.vector, g - 2, GPSIMD_H if g - 2 < GPSIMD_GROUPS - 1 else 0, GROUP)
                 store(g - 2, 0, GROUP, 0, CH)
 
         last = GROUPS - 1

@@ -32,7 +32,7 @@ V5 = True
 IO_SCALAR = (0, 2)
 GPSIMD_GROUPS = 6
 U_FIRST = True
-WARM_UP = 4
+WARM_UP = 6
 HEAD_GROUPS = 3
 FLOPS = 2 * NODES * (SIZE + CH) * 3 * CH
 
@@ -59,7 +59,7 @@ def tile_treelstm_pb_t_kernel(
         fc_dram = fc_sum.rearrange("(p t) k -> p t k", t=TILES)
         out_dram = out.rearrange("(p t) c -> p t c", t=TILES)
 
-        ones = keep.tile([P, BANK], BF16, name="ones")
+        ones = keep.tile([P, CH], BF16, name="ones")
         nc.vector.memset(ones[:], 1.0)
         bias_rows = keep.tile([P, 3 * CH], BF16, name="bias_rows")
         nc.vector.memset(bias_rows[:].bitcast(I32), 0)
@@ -199,7 +199,7 @@ def tile_treelstm_pb_t_kernel(
 
         def leaves_by_scalar(fill):
             kind, unit, j = fill
-            return kind in ("u", "whole") or (kind == "col_mx" and j in IO_SCALAR + ((4,) if V5 else (4, 5)))
+            return kind in ("u", "whole") or (kind == "col_mx" and j in IO_SCALAR + ((4,) if V5 and unit > 2 else (4, 5)))
 
         def turned_block(bank, at, g, t, block, start):
             nc.tensor.matmul(
@@ -363,28 +363,35 @@ def tile_treelstm_pb_t_kernel(
 
         warm_bank = v_bank("warm_bank")
         for n in range(WARM_UP):
-            nc.tensor.matmul(out=warm_bank[:], lhsT=ones[:, 0:P], rhs=ones[:], start=True, stop=True)
-        u_bank = [v_bank("u_bank%d" % j) for j in range(2)]
-        for j in range(2):
+            nc.tensor.matmul(out=warm_bank[:, 0:CH], lhsT=ones[:, 0:P], rhs=ones[:], start=True, stop=True)
+
+        def front_u(j, on_scalar):
+            bank = (s_bank if on_scalar else v_bank)("u_bank%d" % j)
             for b in range(2):
-                turn(u_bank[0], 2 * j + b, words(u_in[j]), b)
-        nc.vector.tensor_copy(out=uT[:, :, 0:BANK], in_=halves(u_bank[0][:]))
+                turn(bank, b, words(u_in[j]), b)
+            copy = nc.scalar.copy if on_scalar else nc.vector.tensor_copy
+            copy(out=uT[:, :, CH * j : CH * (j + 1)], in_=halves(bank[:, 0:CH]))
+
+        front_u(0, False)
+        front_u(1, True)
         front_h(0)
-        for b in range(2):
-            turn(u_bank[1], b, words(u_in[2]), b)
-        nc.vector.tensor_copy(out=uT[:, :, BANK : 3 * CH], in_=halves(u_bank[1][:, 0:CH]))
+        front_u(2, False)
         bias_io = s_bank("bias_io")
         nc.tensor.matmul(out=bias_io[:], lhsT=ones[:, 0:P], rhs=bias_rows[:, 0:BANK], start=True, stop=True)
-        bias_cols_bank = v_bank("bias_cols_bank")
-        for block in range(BLOCKS):
-            nc.tensor.matmul(
-                out=bias_cols_bank[:, block : block + 1],
-                lhsT=bias_rows[:, P * block : P * (block + 1)],
-                rhs=ones[:, 0:1],
-                start=True,
-                stop=True,
-            )
-        bias_u_bank = v_bank("bias_u_bank")
+        nc.scalar.copy(out=bias_all[:], in_=bias_io[:])
+
+        def fill_and_empty(*fills):
+            for fill in fills:
+                tensor_fill(fill)
+            for fill in fills:
+                empty(fill)
+
+        front_w(0)
+        fill_and_empty(("plain", 0, 0))
+        front_w(1)
+        fill_and_empty(("plain", 0, 1))
+        front_z(0, 0)
+        bias_u_bank = s_bank("bias_u_bank")
         for j in range(2):
             nc.tensor.matmul(
                 out=bias_u_bank[:, CH * j : CH * (j + 1)],
@@ -393,23 +400,9 @@ def tile_treelstm_pb_t_kernel(
                 start=True,
                 stop=True,
             )
-        nc.scalar.copy(out=bias_all[:], in_=bias_io[:])
-        nc.vector.tensor_copy(out=bias_cols[:], in_=bias_cols_bank[:, 0:BLOCKS])
-        nc.vector.tensor_copy(out=bias_uu[:], in_=bias_u_bank[:])
-
-        def fill_and_empty(*fills):
-            for fill in fills:
-                tensor_fill(fill)
-            for fill in fills:
-                empty(fill)
-
-        fill_and_empty(("plain", 0, 0))
-        front_w(0)
-        fill_and_empty(("plain", 0, 1))
-        front_w(1)
-        front_z(0, 0)
-        fill_and_empty(("plain_u", 0, 0))
+        nc.scalar.copy(out=bias_uu[:], in_=bias_u_bank[:])
         quantise_w(0, BANK)
+        fill_and_empty(("plain_u", 0, 0))
         front_w(2)
         quantise_z(0, 0, 1)
         fill_and_empty(("plain", 1, 0))
@@ -427,10 +420,21 @@ def tile_treelstm_pb_t_kernel(
         sigmoid_io(0)
         tanh_u(0)
         front_z(2, 0)
+        front_z(2, 1)
+        quantise_z(2)
         sigmoid_io(1)
         tanh_u(1)
-        front_z(2, 1)
         front_h(2)
+        bias_cols_bank = v_bank("bias_cols_bank")
+        for block in range(BLOCKS):
+            nc.tensor.matmul(
+                out=bias_cols_bank[:, block : block + 1],
+                lhsT=bias_rows[:, P * block : P * (block + 1)],
+                rhs=ones[:, 0:1],
+                start=True,
+                stop=True,
+            )
+        nc.vector.tensor_copy(out=bias_cols[:], in_=bias_cols_bank[:, 0:BLOCKS])
 
         for pair in range(1, PAIRS):
             g, second = divmod(pair, 2)
@@ -449,8 +453,6 @@ def tile_treelstm_pb_t_kernel(
                     tensor_fill(("plain_u", pair, 0))
                 if ahead < GROUPS:
                     front_z(ahead, second)
-                    if second:
-                        front_h(ahead)
                 if not whole and not direct_u:
                     fill_and_empty(("u", pair, 0))
                 if not whole:
@@ -460,11 +462,11 @@ def tile_treelstm_pb_t_kernel(
                     if direct_u:
                         empty(("plain_u", pair, 0))
                     tensor_fill(("mx", pair, 1))
-                    if pair == 2:
-                        quantise_z(2)
                     empty(("mx", pair, 0))
                     if direct_u:
                         tensor_fill(("mx_u", pair, 0))
+                    if second and ahead < GROUPS:
+                        front_h(ahead)
                     empty(("mx", pair, 1))
                     if direct_u:
                         empty(("mx_u", pair, 0))
@@ -472,23 +474,30 @@ def tile_treelstm_pb_t_kernel(
                     fill_and_empty(("col_mx", g + 1, 4), ("col_mx", g + 1, 5))
                 if second == IO_AT and g + 1 in WHOLE_GROUPS:
                     fill_and_empty(*[("col_mx", g + 1, block) for block in IO_BLOCKS])
+                if pair == PAIRS - 3:
+                    tanh_c(g - 1, 0, GROUP)
                 if not whole:
                     sigmoid_io(pair)
                     if direct_u:
                         tanh_u(pair)
+            if pair == PAIRS - 3:
+                hidden(nc.vector, g - 2, GPSIMD_H if g - 2 < GPSIMD_GROUPS - 1 else 0, GROUP)
+                store(g - 2, 0, GROUP, 0, CH)
+                hidden(nc.vector, g - 1, 0, GROUP)
+                store(g - 1, 0, GROUP, 0, CH)
             if g == GPSIMD_GROUPS and g < GROUPS - 1:
                 cell(nc.vector if second else nc.gpsimd, g, 2 * second, 2 * second + 2)
             if not second:
                 continue
             if g < GPSIMD_GROUPS:
                 cell(nc.gpsimd, g, 0, GROUP)
-            if g >= 1:
+            if g >= 1 and g != GROUPS - 2:
                 tanh_c(g - 1, 0, GROUP)
                 if g < GPSIMD_GROUPS and GPSIMD_H:
                     hidden(nc.gpsimd, g - 1, 0, GPSIMD_H)
             if 2 < ahead < GROUPS:
                 quantise_z(ahead)
-            if g >= 2:
+            if 2 <= g < GROUPS - 2:
                 hidden(nc.vector, g - 2, GPSIMD_H if g - 2 < GPSIMD_GROUPS - 1 else 0, GROUP)
                 store(g - 2, 0, GROUP, 0, CH)
 

from contextlib import ExitStack

import concourse.mybir as mybir
from concourse.masks import make_identity

F32 = mybir.dt.float32
BF16 = mybir.dt.bfloat16
U32 = mybir.dt.uint32
U8 = mybir.dt.uint8
I32 = mybir.dt.int32
FP8X4 = mybir.dt.float8_e4m3fn_x4
ACT = mybir.ActivationFunctionType
ALU = mybir.AluOpType

P = 128
NODES, SIZE, CH = 4096, 512, 256
TILES = NODES // P
GROUP = 4
GROUPS = TILES // GROUP
PAIRS = TILES // 2
BANK = 512
BLOCKS = 3 * CH // P
IO_BLOCKS = range(0, 4)
U_BLOCKS = range(4, BLOCKS)
WHOLE_GROUPS = (GROUPS - 1,)
V_RING = 4
S_RING = 4
IO_AT = 1
DIRECT_U = (0, 1)
GPSIMD_H = 1
V5 = True
IO_SCALAR = (0, 2)
GPSIMD_GROUPS = 6
U_FIRST = True
WARM_UP = 6
HEAD_GROUPS = 3
FLOPS = 2 * NODES * (SIZE + CH) * 3 * CH


def tile_treelstm_pb_t_kernel(
    tc, z0, h_tilde, fc_sum, W_i, U_i, b_i, W_o, U_o, b_o, W_u, U_u, b_u, out
):
    nc = tc.nc
    with ExitStack() as ctx:
        ctx.enter_context(tc.manual_schedule())
        keep = ctx.enter_context(tc.tile_pool(name="keep", bufs=1))
        front = ctx.enter_context(tc.tile_pool(name="front", bufs=3))
        io_pool = ctx.enter_context(tc.tile_pool(name="io", bufs=4))
        u_pool = ctx.enter_context(tc.tile_pool(name="u", bufs=3))
        u_mx_pool = ctx.enter_context(tc.tile_pool(name="u_mx", bufs=2))
        io_mx_pool = ctx.enter_context(tc.tile_pool(name="io_mx", bufs=1))
        res_pool = ctx.enter_context(tc.tile_pool(name="res", bufs=4))
        tanh_pool = ctx.enter_context(tc.tile_pool(name="tanh", bufs=3))
        v_psum = ctx.enter_context(tc.psum_pool(name="v_ring", bufs=V_RING))
        s_psum = ctx.enter_context(tc.psum_pool(name="s_ring", bufs=S_RING))

        z_dram = z0.rearrange("(p t) k -> p t k", t=TILES)
        h_dram = h_tilde.rearrange("(p t) k -> p t k", t=TILES)
        fc_dram = fc_sum.rearrange("(p t) k -> p t k", t=TILES)
        out_dram = out.rearrange("(p t) c -> p t c", t=TILES)

        ones = keep.tile([P, CH], BF16, name="ones")
        nc.vector.memset(ones[:], 1.0)
        bias_rows = keep.tile([P, 3 * CH], BF16, name="bias_rows")
        nc.vector.memset(bias_rows[:].bitcast(I32), 0)
        for j, b in enumerate((b_i, b_o, b_u)):
            nc.scalar.dma_start(
                out=bias_rows[0:1, CH * j : CH * (j + 1)], in_=b.rearrange("(o n) -> o n", o=1)
            )
        identity = keep.tile([P, P], F32, name="identity")
        make_identity(nc, identity[:])
        warm = keep.tile([P, 8], F32, name="warm")
        nc.vector.memset(warm[:], 0.0)
        nc.scalar.activation(out=warm[:], in_=warm[:], func=ACT.Sigmoid)

        z_in = [keep.tile([P, GROUP, SIZE], BF16, name="z_in%d" % g) for g in range(GROUPS)]
        h_in = [keep.tile([P, GROUP, CH], BF16, name="h_in%d" % g) for g in range(GROUPS)]
        fc_in = [keep.tile([P, GROUP, CH], BF16, name="fc_in%d" % g) for g in range(GROUPS)]
        w_in = [keep.tile([P, 2, SIZE], BF16, name="w_in%d" % j) for j in range(3)]
        u_in = [keep.tile([P, 2, CH], BF16, name="u_in%d" % j) for j in range(3)]

        def load(dst, src, g, t0=0, t1=GROUP):
            nc.sync.dma_start(out=dst[g][:, t0:t1, :], in_=src[:, GROUP * g + t0 : GROUP * g + t1, :])

        def load_weight(dst, src):
            nc.sync.dma_start(out=dst[:], in_=src.rearrange("(b p) k -> p b k", p=P))

        load_weight(u_in[0], U_i)
        load_weight(u_in[1], U_o)
        load(h_in, h_dram, 0)
        load_weight(u_in[2], U_u)
        load_weight(w_in[0], W_i)
        load_weight(w_in[1], W_o)
        load(z_in, z_dram, 0, 0, 2)
        load_weight(w_in[2], W_u)
        load(z_in, z_dram, 0, 2, 4)
        for g in range(1, GROUPS):
            load(z_in, z_dram, g)
            load(h_in, h_dram, g)
            if g >= 2:
                load(fc_in, fc_dram, g - 2)
        load(fc_in, fc_dram, GROUPS - 2)
        load(fc_in, fc_dram, GROUPS - 1)

        def words(tile_ap):
            return tile_ap[:].rearrange("p a k -> p (a k)").bitcast(F32)

        def turn(bank, at, src_words, square):
            nc.tensor.transpose(
                bank[:, P * at : P * (at + 1)], src_words[:, P * square : P * (square + 1)], identity[:]
            )

        def turn_mx(bank, at, src_words):
            w0 = 2 * P * (at // 2) + at % 2
            nc.tensor.transpose(
                bank[:, P * (at % 4) : P * (at % 4 + 1)], src_words[:, w0 : w0 + 2 * P - 1 : 2], identity[:]
            )

        def v_bank(name):
            return v_psum.tile([P, BANK], F32, name=name, tag="v")

        def s_bank(name):
            return s_psum.tile([P, BANK], F32, name=name, tag="s")

        h_bank, z_bank = {}, {}

        def turn_h(g, j):
            if j == 0:
                h_bank[g] = s_bank("h_bank%d" % g)
            turn(h_bank[g], j, words(h_in[g]), j)

        def turn_z(g, half, j):
            if j == 0:
                z_bank[g, half] = s_bank("z_bank%d_%d" % (g, half))
            turn_mx(z_bank[g, half], 4 * half + j, words(z_in[g]))

        def regroup(dst_words, bank):
            nc.scalar.copy(
                out=dst_words.rearrange("p (s m v) -> p s m v", s=2, m=P, v=2),
                in_=bank[:].rearrange("p (s v m) -> p s m v", s=2, v=2, m=P),
            )

        def halves(bank_words):
            return bank_words.bitcast(BF16).rearrange("p (n e) -> p e n", e=2)

        hT, z_grouped, z_codes, z_scales = {}, {}, {}, {}

        def copy_h(g):
            hT[g] = front.tile([P, BANK], F32, name="hT%d" % g, tag="hT")
            nc.scalar.copy(out=hT[g][:], in_=h_bank[g][:])

        def regroup_z(g, half):
            if half == 0:
                z_grouped[g] = front.tile(
                    [P, 4 * BANK], BF16, name="z_grouped%d" % g, tag="zg", align_bytes=64
                )
            regroup(z_grouped[g][:].bitcast(F32)[:, BANK * half : BANK * (half + 1)], z_bank[g, half])

        def quantise_z(g, half0=0, half1=2):
            if half0 == 0:
                z_codes[g] = front.tile([P, BANK], U32, name="z_codes%d" % g, tag="zc", align_bytes=64)
                z_scales[g] = front.tile([P, BANK], U8, name="z_scales%d" % g, tag="zs", align_bytes=64)
            nc.vector.quantize_mx(
                out=z_codes[g][:, 2 * P * half0 : 2 * P * half1].bitcast(FP8X4),
                scales=z_scales[g][:, 2 * P * half0 : 2 * P * half1],
                in_=z_grouped[g][:, 8 * P * half0 : 8 * P * half1],
            )

        def front_h(g):
            for j in range(GROUP):
                turn_h(g, j)
            copy_h(g)

        def front_z(g, half):
            for j in range(4):
                turn_z(g, half, j)
            regroup_z(g, half)

        uT = keep.tile([P, 2, 3 * CH], BF16, name="uT")
        bias_all = keep.tile([P, BANK], F32, name="bias_all")
        bias_uu = keep.tile([P, BANK], F32, name="bias_uu")
        bias_cols = keep.tile([P, BLOCKS], F32, name="bias_cols")
        w_grouped = keep.tile([P, 12 * CH], BF16, name="w_grouped", align_bytes=64)
        w_codes = keep.tile([P, 3 * CH], U32, name="w_codes", align_bytes=64)
        w_scales = keep.tile([P, 3 * CH], U8, name="w_scales", align_bytes=64)

        def front_w(j):
            bank = s_bank("w_bank%d" % j)
            for square in range(4):
                turn_mx(bank, square, words(w_in[j]))
            regroup(w_grouped[:].bitcast(F32)[:, BANK * j : BANK * (j + 1)], bank)

        def quantise_w(c0, c1):
            nc.vector.quantize_mx(
                out=w_codes[:, c0:c1].bitcast(FP8X4), scales=w_scales[:, c0:c1], in_=w_grouped[:, 4 * c0 : 4 * c1]
            )

        sums, gates_io, gates_u, col_mx = {}, {}, {}, {}

        def leaves_by_scalar(fill):
            kind, unit, j = fill
            return kind in ("u", "whole") or (kind == "col_mx" and j in IO_SCALAR + ((4,) if V5 and unit > 2 else (4, 5)))

        def turned_block(bank, at, g, t, block, start):
            nc.tensor.matmul(
                out=bank[:, at : at + P],
                lhsT=col_mx[g, block][:, P * t : P * (t + 1)],
                rhs=identity[:],
                is_transpose=True,
                start=start,
                stop=False,
            )

        def tensor_fill(fill):
            kind, unit, j = fill
            bank = (s_bank if leaves_by_scalar(fill) else v_bank)("sums_%s_%d_%d" % fill)
            sums[fill] = bank
            if kind == "col_mx":
                c0 = P * j
                nc.tensor.matmul_mx(
                    out=bank[:],
                    lhsT=w_codes[:, c0 : c0 + P].bitcast(FP8X4),
                    lhsT_scale=w_scales[:, c0 : c0 + P],
                    rhs=z_codes[unit][:].bitcast(FP8X4),
                    rhs_scale=z_scales[unit][:],
                    start=True,
                    stop=True,
                )
                return
            g, second = divmod(unit, 2)
            t = 2 * second + j
            if kind == "mx":
                nc.tensor.matmul_mx(
                    out=bank[:],
                    lhsT=z_codes[g][:, P * t : P * (t + 1)].bitcast(FP8X4),
                    lhsT_scale=z_scales[g][:, P * t : P * (t + 1)],
                    rhs=w_codes[:, 0:BANK].bitcast(FP8X4),
                    rhs_scale=w_scales[:, 0:BANK],
                    start=True,
                    stop=True,
                )
                return
            h_tile = hT[g][:].bitcast(BF16).rearrange("p (t m e) -> p t m e", t=GROUP, m=P, e=2)
            if kind == "mx_u":
                for t in (2 * second, 2 * second + 1):
                    nc.tensor.matmul_mx(
                        out=bank[:, CH * (t % 2) : CH * (t % 2 + 1)],
                        lhsT=z_codes[g][:, P * t : P * (t + 1)].bitcast(FP8X4),
                        lhsT_scale=z_scales[g][:, P * t : P * (t + 1)],
                        rhs=w_codes[:, BANK : 3 * CH].bitcast(FP8X4),
                        rhs_scale=w_scales[:, BANK : 3 * CH],
                        start=True,
                        stop=True,
                    )
                return
            if kind in ("plain", "whole"):
                if kind == "whole":
                    for block in IO_BLOCKS:
                        turned_block(bank, P * block, g, t, block, block == 0)
                for e in range(2):
                    nc.tensor.matmul(
                        out=bank[:],
                        lhsT=h_tile[:, t, :, e],
                        rhs=uT[:, e, 0:BANK],
                        start=(kind == "plain" and e == 0),
                        stop=(e == 1),
                    )
                return
            for t in (2 * second, 2 * second + 1) if kind == "u" else ():
                for block in U_BLOCKS:
                    at = CH * (t % 2) + P * (block % 2)
                    turned_block(bank, at, g, t, block, at == 0)
            for t in (2 * second, 2 * second + 1):
                for e in range(2):
                    nc.tensor.matmul(
                        out=bank[:, CH * (t % 2) : CH * (t % 2 + 1)],
                        lhsT=h_tile[:, t, :, e],
                        rhs=uT[:, e, BANK : 3 * CH],
                        start=(kind == "plain_u" and e == 0),
                        stop=(e == 1 and (kind == "plain_u" or t % 2 == 1)),
                    )

        def empty(fill):
            kind, unit, j = fill
            bank = sums[fill]
            if kind == "col_mx":
                if j == 0:
                    io_mx = io_mx_pool.tile([P, len(IO_BLOCKS) * BANK], F32, name="io_mx%d" % unit, tag="io_mx")
                    for block in IO_BLOCKS:
                        col_mx[unit, block] = io_mx[:, BANK * block : BANK * (block + 1)]
                if j == 4:
                    u_mx = u_mx_pool.tile([P, len(U_BLOCKS) * BANK], F32, name="u_mx%d" % unit, tag="u_mx")
                    for block in U_BLOCKS:
                        col_mx[unit, block] = u_mx[:, BANK * (block - 4) : BANK * (block - 3)]
                dst = col_mx[unit, j]
                b_col = bias_cols[:, j : j + 1]
                if leaves_by_scalar(fill):
                    nc.scalar.activation(out=dst, in_=bank[:], func=ACT.Identity, bias=b_col)
                else:
                    nc.vector.tensor_scalar(out=dst, in0=bank[:], scalar1=b_col, scalar2=None, op0=ALU.add)
                return
            g, second = divmod(unit, 2)
            if g not in gates_io:
                gates_io[g] = io_pool.tile([P, GROUP * BANK], F32, name="gates_io%d" % g, tag="io")
                gates_u[g] = u_pool.tile([P, GROUP * CH], F32, name="gates_u%d" % g, tag="u")
            if kind == "u":
                dst = gates_u[g][:, BANK * second : BANK * (second + 1)]
                nc.scalar.activation(out=dst, in_=bank[:], func=ACT.Tanh)
                return
            if kind in ("plain_u", "mx_u"):
                dst = gates_u[g][:, BANK * second : BANK * (second + 1)]
                nc.vector.tensor_tensor(
                    out=dst, in0=bank[:], in1=bias_uu[:] if kind == "plain_u" else dst, op=ALU.add
                )
                return
            t = 2 * second + j
            dst = gates_io[g][:, BANK * t : BANK * (t + 1)]
            if kind == "whole":
                nc.scalar.activation(out=dst, in_=bank[:], func=ACT.Sigmoid)
                return
            nc.vector.tensor_tensor(
                out=dst, in0=bank[:], in1=bias_all[:] if kind == "plain" else dst, op=ALU.add
            )

        def tanh_u(pair):
            g, second = divmod(pair, 2)
            v = gates_u[g][:, BANK * second : BANK * (second + 1)]
            nc.scalar.activation(out=v, in_=v, func=ACT.Tanh)

        def sigmoid_io(pair):
            g, second = divmod(pair, 2)
            v = gates_io[g][:, 2 * BANK * second : 2 * BANK * (second + 1)]
            nc.scalar.activation(out=v, in_=v, func=ACT.Sigmoid)

        res, tanh_c_sb = {}, {}

        def cell(engine, g, t0, t1):
            if g not in res:
                res[g] = res_pool.tile([P, GROUP, 2 * CH], F32, name="res%d" % g, tag="res")
                tanh_c_sb[g] = tanh_pool.tile([P, GROUP, CH], F32, name="tanh_c%d" % g, tag="tanh")
            io = gates_io[g][:].rearrange("p (t c) -> p t c", c=BANK)
            uu = gates_u[g][:].rearrange("p (t c) -> p t c", c=CH)
            c = res[g][:, t0:t1, CH : 2 * CH]
            engine.tensor_tensor(out=c, in0=io[:, t0:t1, 0:CH], in1=uu[:, t0:t1, :], op=ALU.mult)
            engine.tensor_tensor(out=c, in0=c, in1=fc_in[g][:, t0:t1, :], op=ALU.add)
            store(g, t0, t1, CH, 2 * CH)

        def tanh_c(g, t0, t1):
            nc.scalar.activation(
                out=tanh_c_sb[g][:, t0:t1, :], in_=res[g][:, t0:t1, CH : 2 * CH], func=ACT.Tanh
            )

        def hidden(engine, g, t0, t1):
            io = gates_io[g][:].rearrange("p (t c) -> p t c", c=BANK)
            engine.tensor_tensor(
                out=res[g][:, t0:t1, 0:CH], in0=io[:, t0:t1, CH:BANK], in1=tanh_c_sb[g][:, t0:t1, :], op=ALU.mult
            )

        def store(g, t0, t1, c0, c1):
            nc.sync.dma_start(
                out=out_dram[:, GROUP * g + t0 : GROUP * g + t1, c0:c1], in_=res[g][:, t0:t1, c0:c1]
            )

        warm_bank = v_bank("warm_bank")
        for n in range(WARM_UP):
            nc.tensor.matmul(out=warm_bank[:, 0:CH], lhsT=ones[:, 0:P], rhs=ones[:], start=True, stop=True)

        def front_u(j, on_scalar):
            bank = (s_bank if on_scalar else v_bank)("u_bank%d" % j)
            for b in range(2):
                turn(bank, b, words(u_in[j]), b)
            copy = nc.scalar.copy if on_scalar else nc.vector.tensor_copy
            copy(out=uT[:, :, CH * j : CH * (j + 1)], in_=halves(bank[:, 0:CH]))

        front_u(0, False)
        front_u(1, True)
        front_h(0)
        front_u(2, False)
        bias_io = s_bank("bias_io")
        nc.tensor.matmul(out=bias_io[:], lhsT=ones[:, 0:P], rhs=bias_rows[:, 0:BANK], start=True, stop=True)
        nc.scalar.copy(out=bias_all[:], in_=bias_io[:])

        def fill_and_empty(*fills):
            for fill in fills:
                tensor_fill(fill)
            for fill in fills:
                empty(fill)

        front_w(0)
        fill_and_empty(("plain", 0, 0))
        front_w(1)
        fill_and_empty(("plain", 0, 1))
        front_z(0, 0)
        bias_u_bank = s_bank("bias_u_bank")
        for j in range(2):
            nc.tensor.matmul(
                out=bias_u_bank[:, CH * j : CH * (j + 1)],
                lhsT=ones[:, 0:P],
                rhs=bias_rows[:, BANK : 3 * CH],
                start=True,
                stop=True,
            )
        nc.scalar.copy(out=bias_uu[:], in_=bias_u_bank[:])
        quantise_w(0, BANK)
        fill_and_empty(("plain_u", 0, 0))
        front_w(2)
        quantise_z(0, 0, 1)
        fill_and_empty(("plain", 1, 0))
        quantise_w(BANK, 3 * CH)
        front_z(0, 1)
        fill_and_empty(("plain", 1, 1))
        quantise_z(0, 1, 2)
        front_z(1, 0)
        fill_and_empty(("mx", 0, 0), ("mx", 0, 1), ("mx_u", 0, 0))
        front_h(1)
        front_z(1, 1)
        fill_and_empty(("plain_u", 1, 0))
        fill_and_empty(("mx", 1, 0), ("mx", 1, 1), ("mx_u", 1, 0))
        quantise_z(1)
        sigmoid_io(0)
        tanh_u(0)
        front_z(2, 0)
        front_z(2, 1)
        quantise_z(2)
        sigmoid_io(1)
        tanh_u(1)
        front_h(2)
        bias_cols_bank = v_bank("bias_cols_bank")
        for block in range(BLOCKS):
            nc.tensor.matmul(
                out=bias_cols_bank[:, block : block + 1],
                lhsT=bias_rows[:, P * block : P * (block + 1)],
                rhs=ones[:, 0:1],
                start=True,
                stop=True,
            )
        nc.vector.tensor_copy(out=bias_cols[:], in_=bias_cols_bank[:, 0:BLOCKS])

        for pair in range(1, PAIRS):
            g, second = divmod(pair, 2)
            ahead = g + 2
            whole = g in WHOLE_GROUPS
            direct_u = g in DIRECT_U
            if pair > 1:
                if whole:
                    fill_and_empty(("u", pair, 0))
                for j in range(2):
                    if whole:
                        fill_and_empty(("whole", pair, j))
                    else:
                        tensor_fill(("plain", pair, j))
                if direct_u:
                    tensor_fill(("plain_u", pair, 0))
                if ahead < GROUPS:
                    front_z(ahead, second)
                if not whole and not direct_u:
                    fill_and_empty(("u", pair, 0))
                if not whole:
                    for j in range(2):
                        empty(("plain", pair, j))
                    tensor_fill(("mx", pair, 0))
                    if direct_u:
                        empty(("plain_u", pair, 0))
                    tensor_fill(("mx", pair, 1))
                    empty(("mx", pair, 0))
                    if direct_u:
                        tensor_fill(("mx_u", pair, 0))
                    if second and ahead < GROUPS:
                        front_h(ahead)
                    empty(("mx", pair, 1))
                    if direct_u:
                        empty(("mx_u", pair, 0))
                if not second and g + 1 < GROUPS and g + 1 not in DIRECT_U:
                    fill_and_empty(("col_mx", g + 1, 4), ("col_mx", g + 1, 5))
                if second == IO_AT and g + 1 in WHOLE_GROUPS:
                    fill_and_empty(*[("col_mx", g + 1, block) for block in IO_BLOCKS])
                if pair == PAIRS - 3:
                    tanh_c(g - 1, 0, GROUP)
                if not whole:
                    sigmoid_io(pair)
                    if direct_u:
                        tanh_u(pair)
            if pair == PAIRS - 3:
                hidden(nc.vector, g - 2, GPSIMD_H if g - 2 < GPSIMD_GROUPS - 1 else 0, GROUP)
                store(g - 2, 0, GROUP, 0, CH)
                hidden(nc.vector, g - 1, 0, GROUP)
                store(g - 1, 0, GROUP, 0, CH)
            if g == GPSIMD_GROUPS and g < GROUPS - 1:
                cell(nc.vector if second else nc.gpsimd, g, 2 * second, 2 * second + 2)
            if not second:
                continue
            if g < GPSIMD_GROUPS:
                cell(nc.gpsimd, g, 0, GROUP)
            if g >= 1 and g != GROUPS - 2:
                tanh_c(g - 1, 0, GROUP)
                if g < GPSIMD_GROUPS and GPSIMD_H:
                    hidden(nc.gpsimd, g - 1, 0, GPSIMD_H)
            if 2 < ahead < GROUPS:
                quantise_z(ahead)
            if 2 <= g < GROUPS - 2:
                hidden(nc.vector, g - 2, GPSIMD_H if g - 2 < GPSIMD_GROUPS - 1 else 0, GROUP)
                store(g - 2, 0, GROUP, 0, CH)

        last = GROUPS - 1
        for t0 in (0, 2):
            cell(nc.vector, last, t0, t0 + 2)
            tanh_c(last, t0, t0 + 2)
        hidden(nc.vector, last - 1, 0, GROUP)
        store(last - 1, 0, GROUP, 0, CH)
        for t0 in (0, 2):
            hidden(nc.vector, last, t0, t0 + 2)
            store(last, t0, t0 + 2, 0, CH)
